import numpy as np
import ml_dtypes


def mxq(x, axis, fmt="e4m3"):
    dtype, down = {"e4m3": (ml_dtypes.float8_e4m3fn, 7), "e5m2": (ml_dtypes.float8_e5m2, 14)}[fmt]
    v = np.moveaxis(np.asarray(x, np.float32).astype(ml_dtypes.bfloat16).astype(np.float64), axis, -1)
    blocks = v.reshape(v.shape[:-1] + (-1, 32))
    amax = np.abs(blocks).max(-1, keepdims=True)
    byte = np.maximum(np.where(amax > 0, np.frexp(amax)[1] - 1 + 127, 0) - down, 1)
    scale = np.exp2(byte - 127.0)
    codes = (blocks / scale).astype(np.float32).astype(dtype).astype(np.float64)
    return np.moveaxis((codes * scale).reshape(v.shape), -1, axis)


WIDE = False


def mx_kscale(k):
    if not WIDE:
        return np.ones(k)
    levels = np.array([10, -10, 5, -5, 0])
    if k % 512:
        return np.exp2(np.random.permutation(np.resize(levels, k // 32))).repeat(32)
    a = np.empty((k // 512, 16))
    for p in range(k // 512):
        a[p, :8] = np.random.permutation(np.resize(levels, 8))
        for g in range(8):
            far = levels[np.abs(levels - a[p, g]) >= 10]
            a[p, g + 8] = far[np.random.randint(len(far))]
    return np.exp2(a.ravel()).repeat(32)


BF16 = ml_dtypes.bfloat16


def bf(x):
    return np.asarray(x, np.float32).astype(BF16)


def f64(x):
    return np.asarray(x).astype(np.float64)


B, S, D = 4, 512, 1024
NB = 2
W = 2 * NB + 1


def setup_inputs():
    s = mx_kscale(D)
    return {"x": bf(np.random.standard_normal((B, S, D)) * s),
            "Wq": bf(np.random.standard_normal((D, D)) / np.sqrt(D) / s[None, :]),
            "bq": bf(np.random.standard_normal(D) * 0.3),
            "k_proj": bf(np.random.standard_normal((B, S, D)))}


def reference(x, Wq, bq, k_proj):
    kf = f64(k_proj)
    q = (mxq(f64(x), 2, "e4m3") @ mxq(f64(Wq), 1, "e4m3").T) + f64(bq)
    scores = np.full((B, S, W), -np.inf)
    for j in range(W):
        o = j - NB
        lo, hi = max(0, -o), S - max(0, o)
        scores[:, lo:hi, j] = (q[:, lo:hi] * kf[:, lo + o:hi + o]).sum(-1) / np.sqrt(D)
    e = np.exp(scores - scores.max(-1, keepdims=True))
    return e / e.sum(-1, keepdims=True)

@@ -1,0 +1,432 @@
+from contextlib import ExitStack
+
+import concourse.mybir as mybir
+from concourse.masks import make_identity
+
+F32 = mybir.dt.float32
+BF16 = mybir.dt.bfloat16
+U32 = mybir.dt.uint32
+U8 = mybir.dt.uint8
+FP8X4 = mybir.dt.float8_e4m3fn_x4
+ALU = mybir.AluOpType
+ACT = mybir.ActivationFunctionType
+AX = mybir.AxisListType
+
+P = 128
+B, S, D = 4, 512, 1024
+W5 = 5
+NV = 4
+VS = 512
+PE_BATCHES = tuple([b for b in range(B) if not VS <= S * b < VS + P * NV])
+KPAD = 8
+KW = S + 2 * KPAD
+NWIN = 132
+MOD = 6
+BIG = 1.0e30
+
+FLOPS = 2 * B * S * D * D + 2 * B * S * W5 * D
+
+
+def tile_crosssliceattention_pa_kernel(tc, x, Wq, bq, k_proj, out):
+    nc = tc.nc
+    xf = x.flatten_outer_dims()
+    kf = k_proj.flatten_outer_dims()
+    of = out.flatten_outer_dims()
+
+    with ExitStack() as ctx:
+        consts = ctx.enter_context(tc.tile_pool(name="consts", bufs=1))
+        rawp = ctx.enter_context(tc.tile_pool(name="raw", bufs=1))
+        gp = ctx.enter_context(tc.tile_pool(name="grouped", bufs=2))
+        ktp = ctx.enter_context(tc.tile_pool(name="kt", bufs=2))
+        qtp = ctx.enter_context(tc.tile_pool(name="qt", bufs=2))
+        codes = ctx.enter_context(tc.tile_pool(name="codes", bufs=1))
+        work = ctx.enter_context(tc.tile_pool(name="work", bufs=2))
+        small = ctx.enter_context(tc.tile_pool(name="small", bufs=1))
+        tp = ctx.enter_context(tc.psum_pool(name="banks", bufs=6))
+        sp = ctx.enter_context(tc.psum_pool(name="sps", bufs=2))
+        ctx.enter_context(tc.manual_schedule())
+
+        brow = consts.tile([P, 2 * P], BF16)
+        nc.vector.memset(brow[:], 0.0)
+        nc.sync.dma_start(out=brow[0:4, :], in_=bq.rearrange("(u w) -> u w", u=4))
+
+        w_raw = rawp.tile([P, 4, 2, D], BF16, tag="big")
+        wv = Wq.rearrange("(u p e) i -> p u e i", p=P, e=2)
+        xraw = {}
+        kraw = {}
+
+        def load_w(u):
+            nc.sync.dma_start(out=w_raw[:, u, :, :], in_=wv[:, u, :, :])
+
+        def load_x(key, view):
+            xr = rawp.tile([P, 4, D], BF16, tag="xr", bufs=3)
+            for hh in range(2):
+                nc.sync.dma_start(out=xr[:, 2 * hh : 2 * hh + 2, :], in_=view[:, 2 * hh : 2 * hh + 2, :])
+            xraw[key] = xr
+
+        def load_xv(vg):
+            view = xf[VS : VS + P * NV, :].rearrange("(p r) i -> p r i", r=NV)
+            load_x("v%d" % vg, view[:, 4 * vg : 4 * vg + 4, :])
+
+        def load_xp(b):
+            load_x("p%d" % b, xf[S * b : S * (b + 1), :].rearrange("(t p) i -> p t i", p=P))
+
+        def load_k(b):
+            kr = rawp.tile([P, 4, D], BF16, name="kraw%d" % b)
+            view = kf[S * b : S * (b + 1), :].rearrange("(t p) d -> p t d", p=P)
+            for hh in range(2):
+                nc.sync.dma_start(out=kr[:, 2 * hh : 2 * hh + 2, :], in_=view[:, 2 * hh : 2 * hh + 2, :])
+            kraw[b] = kr
+
+        load_w(0)
+        load_w(1)
+        load_xv(0)
+        load_w(2)
+        load_w(3)
+        for vg in range(1, NV // 4):
+            load_xv(vg)
+        load_xp(PE_BATCHES[0])
+        load_k(PE_BATCHES[0])
+        k_v = rawp.tile([P, NV + 4, D], BF16)
+        base = VS - 2
+        nc.sync.dma_start(
+            out=k_v[:, 0:NV, :], in_=kf[base : base + P * NV, :].rearrange("(p c) d -> p c d", c=NV)
+        )
+        nc.sync.dma_start(
+            out=k_v[:, NV : NV + 4, :],
+            in_=kf[base + NV : base + NV + P * NV, :].rearrange("(p c) d -> p c d", c=NV)[:, 0:4, :],
+        )
+        for b in PE_BATCHES[1:-1]:
+            load_xp(b)
+            load_k(b)
+
+        ident = consts.tile([P, P], F32)
+        make_identity(nc, ident[:])
+        warm = consts.tile([P, 1], F32)
+        nc.gpsimd.memset(warm[:], 0.0)
+        warm2 = consts.tile([P, 1], F32)
+        nc.scalar.activation(out=warm2[:], in_=warm[:], func=ACT.Exp)
+
+        bt = tp.tile([P, 4, P], F32, tag="tp")
+        nc.tensor.transpose(bt[:, 0, :], brow[:].bitcast(F32), ident[:])
+        bw = consts.tile([P, 4], F32)
+        nc.vector.tensor_copy(out=bw[:], in_=bt[:, 0, 0:4])
+        rep = consts.tile([P, 4, P], F32)
+        nc.vector.tensor_copy(out=rep[:], in_=bw[:].unsqueeze(2).to_broadcast([P, 4, P]))
+        bbank = tp.tile([P, 4, P], F32, tag="tp")
+        for u in range(4):
+            nc.tensor.transpose(bbank[:, u, :], rep[:, u, :], ident[:])
+        bb = consts.tile([P, D], BF16)
+        nc.vector.tensor_copy(out=bb[:].bitcast(F32), in_=bbank[:].rearrange("p u w -> p (u w)"))
+        bpp = consts.tile([P, 8], F32)
+        nc.vector.tensor_copy(out=bpp[:], in_=bw[:].bitcast(BF16))
+
+        band = consts.tile([P, NWIN], F32)
+        nc.gpsimd.memset(band[:], 0.0)
+        for j in range(W5):
+            nc.gpsimd.tensor_tensor(out=band[:, j : j + P], in0=band[:, j : j + P], in1=ident[:], op=ALU.add)
+        idw = consts.tile([P, NWIN], F32)
+        nc.gpsimd.memset(idw[:], 0.0)
+        nc.gpsimd.tensor_copy(out=idw[:, 0:P], in_=ident[:])
+        ind = consts.tile([P, MOD], F32)
+        nc.vector.tensor_reduce(out=ind[:], in_=idw[:].rearrange("p (m r) -> p r m", r=MOD), axis=AX.X, op=ALU.add)
+        sel = consts.tile([P, 4, W5, MOD + 1], F32)
+        nc.gpsimd.memset(sel[:], 0.0)
+        for j in range(W5):
+            nc.gpsimd.tensor_copy(
+                out=sel[:, :, j, j:MOD], in_=ind[:, 0 : MOD - j].unsqueeze(1).to_broadcast([P, 4, MOD - j])
+            )
+            if j > 0:
+                nc.gpsimd.tensor_copy(
+                    out=sel[:, :, j, 0:j], in_=ind[:, MOD - j : MOD].unsqueeze(1).to_broadcast([P, 4, j])
+                )
+        for tb, j, c in ((0, 0, 1), (0, 1, 0), (3, 3, NWIN - 1), (3, 4, NWIN - 2)):
+            nc.gpsimd.tensor_scalar(
+                out=sel[:, tb, j, MOD : MOD + 1], in0=band[:, c : c + 1], scalar1=-BIG, scalar2=0.0, op0=ALU.mult, op1=ALU.add
+            )
+        negv = consts.tile([P, NV, W5], F32)
+        nc.gpsimd.memset(negv[:], 0.0)
+        for r, j0, j1, p in ((0, 0, 2, 0), (1, 0, 1, 0), (2, 4, 5, P - 1), (3, 3, 5, P - 1)):
+            nc.gpsimd.tensor_scalar(
+                out=negv[:, r, j0:j1],
+                in0=ident[:, p : p + 1].to_broadcast([P, j1 - j0]),
+                scalar1=-BIG,
+                scalar2=0.0,
+                op0=ALU.mult,
+                op1=ALU.add,
+            )
+        rr = small.tile([P, 16, MOD + 1], F32)
+        nc.gpsimd.memset(rr[:], 0.0)
+        nc.gpsimd.memset(rr[:, :, MOD : MOD + 1], 1.0)
+        sc = small.tile([P, 16, W5], F32)
+        nc.gpsimd.memset(sc[:], 0.0)
+        ypad = small.tile([P, W5, P], F32)
+        nc.gpsimd.memset(ypad[:], 0.0)
+
+        def evac(eng, out_ap, in_ap):
+            if eng == "v":
+                nc.vector.tensor_copy(out=out_ap, in_=in_ap)
+            else:
+                nc.scalar.copy(out=out_ap, in_=in_ap)
+
+        def transpose_words(words):
+            bank = tp.tile([P, 4, P], F32, tag="tp")
+            for blk in range(4):
+                nc.tensor.transpose(bank[:, blk, :], words[:, P * blk : P * (blk + 1)], ident[:])
+            return bank
+
+        def transpose_mx(words):
+            bank = tp.tile([P, 4, P], F32, tag="tp")
+            for g in range(2):
+                for u in range(2):
+                    nc.tensor.transpose(
+                        bank[:, 2 * g + u, :], words[:, 2 * P * g + u : 2 * P * (g + 1) : 2], ident[:]
+                    )
+            return bank
+
+        wc = codes.tile([P, 2, D], U32, align_bytes=64)
+        ws = codes.tile([P, 2, D], U8, align_bytes=64)
+        gw = ktp.tile([P, 2, 4 * D], BF16, tag="kt", align_bytes=64)
+        gwf = gw[:].bitcast(F32).rearrange("p g (c u) -> p g c u", u=2)
+        ww = w_raw[:].bitcast(F32)
+        xc = {}
+        xs = {}
+        grp = {}
+        kts = {}
+        qts = {}
+        spt = {}
+
+        def w_bank(c, eng):
+            bank = transpose_mx(ww[:, c // 2, c % 2, :])
+            evac(eng, gwf[:, :, P * c : P * (c + 1), :], bank[:].rearrange("p (g u) c -> p g c u", u=2))
+
+        def w_quant(h):
+            for g in range(2):
+                nc.vector.quantize_mx(
+                    out=wc[:, g, 512 * h : 512 * (h + 1)].bitcast(FP8X4),
+                    scales=ws[:, g, 512 * h : 512 * (h + 1)],
+                    in_=gw[:, g, 2048 * h : 2048 * (h + 1)],
+                )
+
+        def x_bank(key, j, eng):
+            if j == 0:
+                gt = gp.tile([P, 2, 4 * S], BF16, tag="g", align_bytes=64)
+                grp[key] = gt
+            gf = grp[key][:].bitcast(F32).rearrange("p g (c u) -> p g c u", u=2)
+            bank = transpose_mx(xraw[key][:].bitcast(F32)[:, j, :])
+            evac(eng, gf[:, :, P * j : P * (j + 1), :], bank[:].rearrange("p (g u) c -> p g c u", u=2))
+
+        def x_quant(key):
+            xcb = codes.tile([P, 2, S], U32, name="xc" + key, align_bytes=64)
+            xsb = codes.tile([P, 2, S], U8, name="xs" + key, align_bytes=64)
+            for g in range(2):
+                nc.vector.quantize_mx(out=xcb[:, g, :].bitcast(FP8X4), scales=xsb[:, g, :], in_=grp[key][:, g, :])
+            xc[key] = xcb
+            xs[key] = xsb
+
+        def k_bank(b, tb, eng):
+            if tb == 0:
+                kt = ktp.tile([P, 8, KW], F32, tag="kt", align_bytes=64)
+                nc.gpsimd.memset(kt[:, :, 0:KPAD], 0.0)
+                nc.gpsimd.memset(kt[:, :, KPAD + S : KW], 0.0)
+                kts[b] = kt
+            bank = transpose_words(kraw[b][:].bitcast(F32)[:, tb, :])
+            lo = KPAD + P * tb
+            evac(
+                eng,
+                kts[b][:, :, lo : lo + P].rearrange("p (u e) k -> p u e k", e=2),
+                bank[:].bitcast(BF16).rearrange("p u (k e) -> p u e k", e=2),
+            )
+
+        scv = small.tile([P, NV, W5], F32)
+        vdone = [0]
+
+        def mxv_group(r, h):
+            key = "v%d" % (r // 4)
+            cols = slice(P * (r % 4), P * (r % 4 + 1))
+            qv = tp.tile([P, 512], F32, tag="tp")
+            for g in range(2):
+                nc.tensor.matmul_mx(
+                    out=qv[:],
+                    lhsT=xc[key][:, g, cols].bitcast(FP8X4),
+                    lhsT_scale=xs[key][:, g, cols],
+                    rhs=wc[:, g, 512 * h : 512 * (h + 1)].bitcast(FP8X4),
+                    rhs_scale=ws[:, g, 512 * h : 512 * (h + 1)],
+                    start=(g == 0),
+                    stop=(g == 1),
+                )
+            nc.vector.tensor_tensor(
+                out=qb[:, r, 512 * h : 512 * (h + 1)].rearrange("p (u q e) -> p u q e", u=2, e=2),
+                in0=qv[:].rearrange("p (u e q) -> p u q e", u=2, e=2),
+                in1=bb[:, 512 * h : 512 * (h + 1)].rearrange("p (u q e) -> p u q e", u=2, e=2),
+                op=ALU.add,
+            )
+
+        def softmax(sc_t, groups, dest, label):
+            mx = small.tile([P, groups], F32, name="mx" + label)
+            nc.vector.tensor_reduce(out=mx[:], in_=sc_t[:], axis=AX.X, op=ALU.max)
+            nc.vector.tensor_tensor(
+                out=sc_t[:], in0=sc_t[:], in1=mx[:].unsqueeze(2).to_broadcast([P, groups, W5]), op=ALU.subtract
+            )
+            ex = small.tile([P, groups, W5], F32, name="ex" + label)
+            nc.scalar.activation(out=ex[:], in_=sc_t[:], func=ACT.Exp, scale=1.0 / 32.0)
+            sm = small.tile([P, groups], F32, name="sm" + label)
+            nc.vector.tensor_reduce(out=sm[:], in_=ex[:], axis=AX.X, op=ALU.add)
+            rs = small.tile([P, groups], F32, name="rs" + label)
+            nc.vector.reciprocal(out=rs[:], in_=sm[:])
+            nc.vector.tensor_tensor(
+                out=dest, in0=ex[:], in1=rs[:].unsqueeze(2).to_broadcast([P, groups, W5]), op=ALU.mult
+            )
+
+        def vfill(n):
+            for i in range(n):
+                if vdone[0] >= W5 * NV:
+                    return
+                r, j = divmod(vdone[0], W5)
+                junk = work.tile([P, D], F32, tag="junk", bufs=3)
+                nc.vector.scalar_tensor_tensor(
+                    out=junk[:],
+                    in0=qb[:, r, :],
+                    scalar=1.0,
+                    in1=k_v[:, r + j, :],
+                    op0=ALU.mult,
+                    op1=ALU.mult,
+                    accum_out=scv[:, r, j : j + 1],
+                )
+                vdone[0] += 1
+                if vdone[0] == W5 * NV:
+                    nc.vector.tensor_tensor(out=scv[:], in0=scv[:], in1=negv[:], op=ALU.add)
+                    yv = small.tile([P, NV, W5], F32)
+                    softmax(scv, NV, yv[:], "v")
+                    nc.sync.dma_start(
+                        out=of[VS : VS + P * NV, :].rearrange("(p r) j -> p (r j)", r=NV),
+                        in_=yv[:].rearrange("p r j -> p (r j)"),
+                    )
+
+        def mxp_group(b, c):
+            key = "p%d" % b
+            if c == 0:
+                qt_sb = qtp.tile([P, 8, S], F32, tag="qt")
+                qts[b] = qt_sb
+            qt = tp.tile([P, 512], F32, tag="tp")
+            for g in range(2):
+                nc.tensor.matmul_mx(
+                    out=qt[:],
+                    lhsT=wc[:, g, P * c : P * (c + 1)].bitcast(FP8X4),
+                    lhsT_scale=ws[:, g, P * c : P * (c + 1)],
+                    rhs=xc[key][:, g, :].bitcast(FP8X4),
+                    rhs_scale=xs[key][:, g, :],
+                    start=(g == 0),
+                    stop=(g == 1),
+                )
+            nc.scalar.activation(out=qts[b][:, c, :], in_=qt[:], func=ACT.Identity, bias=bpp[:, c : c + 1], scale=1.0)
+
+        def sc_tile(b, tb):
+            if tb % 2 == 0:
+                sps = sp.tile([P, 2, NWIN], F32, tag="s")
+                spt[b] = sps
+            lo = KPAD - 2 + P * tb
+            for c in range(8):
+                nc.tensor.matmul(
+                    out=spt[b][:, tb % 2, :],
+                    lhsT=qts[b][:, c, P * tb : P * (tb + 1)],
+                    rhs=kts[b][:, c, lo : lo + NWIN],
+                    start=(c == 0),
+                    stop=(c == 7),
+                )
+
+        def ex_half(b, half):
+            bm = work.tile([P, 2, NWIN], F32, tag="bm")
+            nc.vector.tensor_tensor(
+                out=bm[:], in0=spt[b][:], in1=band[:].unsqueeze(1).to_broadcast([P, 2, NWIN]), op=ALU.mult
+            )
+            slot = 4 * b + 2 * half
+            nc.vector.tensor_reduce(
+                out=rr[:, slot : slot + 2, 0:MOD],
+                in_=bm[:].rearrange("p t (m r) -> p t r m", r=MOD),
+                axis=AX.X,
+                op=ALU.add,
+            )
+            pr = work.tile([P, 2, W5, MOD + 1], F32, tag="pr")
+            nc.vector.tensor_tensor(
+                out=pr[:],
+                in0=rr[:, slot : slot + 2, :].unsqueeze(2).to_broadcast([P, 2, W5, MOD + 1]),
+                in1=sel[:, 2 * half : 2 * half + 2, :, :],
+                op=ALU.mult,
+            )
+            nc.vector.tensor_reduce(out=sc[:, slot : slot + 2, :], in_=pr[:], axis=AX.X, op=ALU.add)
+
+        for c in range(4):
+            w_bank(c, "s")
+        w_quant(0)
+        for j in range(4):
+            x_bank("v0", j, "s")
+        x_quant("v0")
+        load_xp(PE_BATCHES[-1])
+        load_k(PE_BATCHES[-1])
+        for c in range(4, 8):
+            w_bank(c, "s")
+        w_quant(1)
+        qb = rawp.tile([P, NV, D], F32, tag="big")
+        for vg in range(1, NV // 4):
+            for j in range(4):
+                x_bank("v%d" % vg, j, "s")
+            x_quant("v%d" % vg)
+        first = PE_BATCHES[0]
+        for r in range(4):
+            mxv_group(r, 0)
+        for j in range(4):
+            x_bank("p%d" % first, j, "s")
+        x_quant("p%d" % first)
+        for tb in range(4):
+            k_bank(first, tb, "s")
+        for r in range(4):
+            mxv_group(r, 1)
+        for r in range(4, NV):
+            mxv_group(r, 0)
+            mxv_group(r, 1)
+        for c in range(8):
+            mxp_group(first, c)
+        vfill(3)
+
+        for gi, b in enumerate(PE_BATCHES):
+            nxt = PE_BATCHES[gi + 1] if gi + 1 < len(PE_BATCHES) else None
+            nkey = "p%d" % nxt if nxt is not None else ""
+            sc_tile(b, 0)
+            if nxt is not None:
+                for j in range(3):
+                    x_bank(nkey, j, "s")
+            vfill(2)
+            sc_tile(b, 1)
+            if nxt is not None:
+                x_bank(nkey, 3, "s")
+                k_bank(nxt, 0, "s")
+                k_bank(nxt, 1, "s")
+                x_quant(nkey)
+            ex_half(b, 0)
+            vfill(2)
+            sc_tile(b, 2)
+            if nxt is not None:
+                k_bank(nxt, 2, "s")
+                k_bank(nxt, 3, "s")
+            sc_tile(b, 3)
+            ex_half(b, 1)
+            if nxt is not None:
+                for c in range(8):
+                    mxp_group(nxt, c)
+                vfill(3)
+
+        softmax(sc, 16, ypad[:, :, 0:16].rearrange("p j t -> p t j"), "p")
+
+        ta = tp.tile([P, 4, P], F32, tag="tp")
+        for j in range(4):
+            nc.tensor.transpose(ta[:, j, :], ypad[:, j, :], ident[:])
+        tb4 = tp.tile([P, 4, P], F32, tag="tp")
+        nc.tensor.transpose(tb4[:, 0, :], ypad[:, 4, :], ident[:])
+        z2 = small.tile([P, P, W5], F32)
+        nc.vector.tensor_copy(out=z2[:, :, 0:4], in_=ta[:].rearrange("s j p -> s p j"))
+        nc.vector.tensor_copy(out=z2[:, :, 4:5], in_=tb4[:, 0:1, :].rearrange("s j p -> s p j"))
+        ov = of.rearrange("(t p) j -> t (p j)", p=P)
+        for b in PE_BATCHES:
+            nc.sync.dma_start(out=ov[4 * b : 4 * b + 4, :], in_=z2[4 * b : 4 * b + 4, :, :].rearrange("s p j -> s (p j)"))
+        vfill(W5 * NV)

@@ -48,7 +48,6 @@ def tile_crosssliceattention_pa_kernel(tc, x, Wq, bq, k_proj, out):
 
         brow = consts.tile([P, 2 * P], BF16)
         nc.vector.memset(brow[:], 0.0)
-        nc.sync.dma_start(out=brow[0:4, :], in_=bq.rearrange("(u w) -> u w", u=4))
 
         w_raw = rawp.tile([P, 4, 2, D], BF16, tag="big")
         wv = Wq.rearrange("(u p e) i -> p u e i", p=P, e=2)
@@ -80,6 +79,7 @@ def tile_crosssliceattention_pa_kernel(tc, x, Wq, bq, k_proj, out):
 
         load_w(0)
         load_w(1)
+        nc.sync.dma_start(out=brow[0:4, :], in_=bq.rearrange("(u w) -> u w", u=4))
         load_xv(0)
         load_w(2)
         load_w(3)
@@ -107,43 +107,16 @@ def tile_crosssliceattention_pa_kernel(tc, x, Wq, bq, k_proj, out):
         warm2 = consts.tile([P, 1], F32)
         nc.scalar.activation(out=warm2[:], in_=warm[:], func=ACT.Exp)
 
-        bt = tp.tile([P, 4, P], F32, tag="tp")
-        nc.tensor.transpose(bt[:, 0, :], brow[:].bitcast(F32), ident[:])
-        bw = consts.tile([P, 4], F32)
-        nc.vector.tensor_copy(out=bw[:], in_=bt[:, 0, 0:4])
-        rep = consts.tile([P, 4, P], F32)
-        nc.vector.tensor_copy(out=rep[:], in_=bw[:].unsqueeze(2).to_broadcast([P, 4, P]))
-        bbank = tp.tile([P, 4, P], F32, tag="tp")
-        for u in range(4):
-            nc.tensor.transpose(bbank[:, u, :], rep[:, u, :], ident[:])
-        bb = consts.tile([P, D], BF16)
-        nc.vector.tensor_copy(out=bb[:].bitcast(F32), in_=bbank[:].rearrange("p u w -> p (u w)"))
-        bpp = consts.tile([P, 8], F32)
-        nc.vector.tensor_copy(out=bpp[:], in_=bw[:].bitcast(BF16))
-
         band = consts.tile([P, NWIN], F32)
         nc.gpsimd.memset(band[:], 0.0)
         for j in range(W5):
             nc.gpsimd.tensor_tensor(out=band[:, j : j + P], in0=band[:, j : j + P], in1=ident[:], op=ALU.add)
         idw = consts.tile([P, NWIN], F32)
         nc.gpsimd.memset(idw[:], 0.0)
-        nc.gpsimd.tensor_copy(out=idw[:, 0:P], in_=ident[:])
+        nc.gpsimd.tensor_scalar(
+            out=idw[:, 0:P], in0=ident[:], scalar1=-1.0 / 32.0, scalar2=0.0, op0=ALU.mult, op1=ALU.add
+        )
         ind = consts.tile([P, MOD], F32)
-        nc.vector.tensor_reduce(out=ind[:], in_=idw[:].rearrange("p (m r) -> p r m", r=MOD), axis=AX.X, op=ALU.add)
-        sel = consts.tile([P, 4, W5, MOD + 1], F32)
-        nc.gpsimd.memset(sel[:], 0.0)
-        for j in range(W5):
-            nc.gpsimd.tensor_copy(
-                out=sel[:, :, j, j:MOD], in_=ind[:, 0 : MOD - j].unsqueeze(1).to_broadcast([P, 4, MOD - j])
-            )
-            if j > 0:
-                nc.gpsimd.tensor_copy(
-                    out=sel[:, :, j, 0:j], in_=ind[:, MOD - j : MOD].unsqueeze(1).to_broadcast([P, 4, j])
-                )
-        for tb, j, c in ((0, 0, 1), (0, 1, 0), (3, 3, NWIN - 1), (3, 4, NWIN - 2)):
-            nc.gpsimd.tensor_scalar(
-                out=sel[:, tb, j, MOD : MOD + 1], in0=band[:, c : c + 1], scalar1=-BIG, scalar2=0.0, op0=ALU.mult, op1=ALU.add
-            )
         negv = consts.tile([P, NV, W5], F32)
         nc.gpsimd.memset(negv[:], 0.0)
         for r, j0, j1, p in ((0, 0, 2, 0), (1, 0, 1, 0), (2, 4, 5, P - 1), (3, 3, 5, P - 1)):
@@ -160,8 +133,11 @@ def tile_crosssliceattention_pa_kernel(tc, x, Wq, bq, k_proj, out):
         nc.gpsimd.memset(rr[:, :, MOD : MOD + 1], 1.0)
         sc = small.tile([P, 16, W5], F32)
         nc.gpsimd.memset(sc[:], 0.0)
-        ypad = small.tile([P, W5, P], F32)
-        nc.gpsimd.memset(ypad[:], 0.0)
+        ypads = {}
+        for part in ("a", "b"):
+            yp = small.tile([P, W5, P], F32, name="ypad" + part)
+            nc.gpsimd.memset(yp[:], 0.0)
+            ypads[part] = yp
 
         def evac(eng, out_ap, in_ap):
             if eng == "v":
@@ -194,7 +170,6 @@ def tile_crosssliceattention_pa_kernel(tc, x, Wq, bq, k_proj, out):
         grp = {}
         kts = {}
         qts = {}
-        spt = {}
 
         def w_bank(c, eng):
             bank = transpose_mx(ww[:, c // 2, c % 2, :])
@@ -262,14 +237,14 @@ def tile_crosssliceattention_pa_kernel(tc, x, Wq, bq, k_proj, out):
                 op=ALU.add,
             )
 
-        def softmax(sc_t, groups, dest, label):
+        def softmax(sc_t, groups, dest, label, extreme, scale):
             mx = small.tile([P, groups], F32, name="mx" + label)
-            nc.vector.tensor_reduce(out=mx[:], in_=sc_t[:], axis=AX.X, op=ALU.max)
+            nc.vector.tensor_reduce(out=mx[:], in_=sc_t, axis=AX.X, op=extreme)
             nc.vector.tensor_tensor(
-                out=sc_t[:], in0=sc_t[:], in1=mx[:].unsqueeze(2).to_broadcast([P, groups, W5]), op=ALU.subtract
+                out=sc_t, in0=sc_t, in1=mx[:].unsqueeze(2).to_broadcast([P, groups, W5]), op=ALU.subtract
             )
             ex = small.tile([P, groups, W5], F32, name="ex" + label)
-            nc.scalar.activation(out=ex[:], in_=sc_t[:], func=ACT.Exp, scale=1.0 / 32.0)
+            nc.scalar.activation(out=ex[:], in_=sc_t, func=ACT.Exp, scale=scale)
             sm = small.tile([P, groups], F32, name="sm" + label)
             nc.vector.tensor_reduce(out=sm[:], in_=ex[:], axis=AX.X, op=ALU.add)
             rs = small.tile([P, groups], F32, name="rs" + label)
@@ -297,7 +272,7 @@ def tile_crosssliceattention_pa_kernel(tc, x, Wq, bq, k_proj, out):
                 if vdone[0] == W5 * NV:
                     nc.vector.tensor_tensor(out=scv[:], in0=scv[:], in1=negv[:], op=ALU.add)
                     yv = small.tile([P, NV, W5], F32)
-                    softmax(scv, NV, yv[:], "v")
+                    softmax(scv[:], NV, yv[:], "v", ALU.max, 1.0 / 32.0)
                     nc.sync.dma_start(
                         out=of[VS : VS + P * NV, :].rearrange("(p r) j -> p (r j)", r=NV),
                         in_=yv[:].rearrange("p r j -> p (r j)"),
@@ -321,51 +296,100 @@ def tile_crosssliceattention_pa_kernel(tc, x, Wq, bq, k_proj, out):
                 )
             nc.scalar.activation(out=qts[b][:, c, :], in_=qt[:], func=ACT.Identity, bias=bpp[:, c : c + 1], scale=1.0)
 
-        def sc_tile(b, tb):
-            if tb % 2 == 0:
-                sps = sp.tile([P, 2, NWIN], F32, tag="s")
-                spt[b] = sps
+        def new_scores():
+            sps = sp.tile([P, 2, NWIN], F32, tag="s")
+            return sps
+
+        def score(b, tb, sps, at):
             lo = KPAD - 2 + P * tb
             for c in range(8):
                 nc.tensor.matmul(
-                    out=spt[b][:, tb % 2, :],
+                    out=sps[:, at, :],
                     lhsT=qts[b][:, c, P * tb : P * (tb + 1)],
                     rhs=kts[b][:, c, lo : lo + NWIN],
                     start=(c == 0),
                     stop=(c == 7),
                 )
 
-        def ex_half(b, half):
+        def extract(b, tb, n, sps):
             bm = work.tile([P, 2, NWIN], F32, tag="bm")
             nc.vector.tensor_tensor(
-                out=bm[:], in0=spt[b][:], in1=band[:].unsqueeze(1).to_broadcast([P, 2, NWIN]), op=ALU.mult
+                out=bm[:, 0:n, :],
+                in0=sps[:, 0:n, :],
+                in1=band[:].unsqueeze(1).to_broadcast([P, n, NWIN]),
+                op=ALU.mult,
             )
-            slot = 4 * b + 2 * half
+            slot = 4 * b + tb
             nc.vector.tensor_reduce(
-                out=rr[:, slot : slot + 2, 0:MOD],
-                in_=bm[:].rearrange("p t (m r) -> p t r m", r=MOD),
+                out=rr[:, slot : slot + n, 0:MOD],
+                in_=bm[:, 0:n, :].rearrange("p t (m r) -> p t r m", r=MOD),
                 axis=AX.X,
                 op=ALU.add,
             )
             pr = work.tile([P, 2, W5, MOD + 1], F32, tag="pr")
             nc.vector.tensor_tensor(
-                out=pr[:],
-                in0=rr[:, slot : slot + 2, :].unsqueeze(2).to_broadcast([P, 2, W5, MOD + 1]),
-                in1=sel[:, 2 * half : 2 * half + 2, :, :],
+                out=pr[:, 0:n, :, :],
+                in0=rr[:, slot : slot + n, :].unsqueeze(2).to_broadcast([P, n, W5, MOD + 1]),
+                in1=sel[:, tb : tb + n, :, :],
                 op=ALU.mult,
             )
-            nc.vector.tensor_reduce(out=sc[:, slot : slot + 2, :], in_=pr[:], axis=AX.X, op=ALU.add)
+            nc.vector.tensor_reduce(out=sc[:, slot : slot + n, :], in_=pr[:, 0:n, :, :], axis=AX.X, op=ALU.add)
+
+        ov = of.rearrange("(t p) j -> t (p j)", p=P)
+
+        def turn(part):
+            yp = ypads[part]
+            ta = tp.tile([P, 4, P], F32, tag="tp")
+            tb2 = tp.tile([P, 4, P], F32, tag="tp")
+            for j in range(W5):
+                nc.tensor.transpose(ta[:, j, :] if j < 3 else tb2[:, j - 3, :], yp[:, j, :], ident[:])
+            zj = small.tile([P, W5, P], F32, name="zj" + part)
+            nc.scalar.copy(out=zj[:, 3:5, :], in_=tb2[:, 0:2, :])
+            if part == "a":
+                nc.scalar.copy(out=zj[:, 0:3, :], in_=ta[:, 0:3, :])
+            else:
+                nc.vector.tensor_copy(out=zj[:, 0:3, :], in_=ta[:, 0:3, :])
+            return zj
 
         for c in range(4):
-            w_bank(c, "s")
+            w_bank(c, "sv"[c % 2])
+        bt = tp.tile([P, 4, P], F32, tag="tp")
+        nc.tensor.transpose(bt[:, 0, :], brow[:].bitcast(F32), ident[:])
+        bw = consts.tile([P, 4], F32)
+        nc.vector.tensor_copy(out=bw[:], in_=bt[:, 0, 0:4])
+        rep = consts.tile([P, 4, P], F32)
+        nc.vector.tensor_copy(out=rep[:], in_=bw[:].unsqueeze(2).to_broadcast([P, 4, P]))
+        bpp = consts.tile([P, 8], F32)
+        nc.vector.tensor_copy(out=bpp[:], in_=bw[:].bitcast(BF16))
+
         w_quant(0)
         for j in range(4):
-            x_bank("v0", j, "s")
+            x_bank("v0", j, "sv"[j % 2])
+        bbank = tp.tile([P, 4, P], F32, tag="tp")
+        for u in range(4):
+            nc.tensor.transpose(bbank[:, u, :], rep[:, u, :], ident[:])
+        bb = consts.tile([P, D], BF16)
+        nc.vector.tensor_copy(out=bb[:].bitcast(F32), in_=bbank[:].rearrange("p u w -> p (u w)"))
         x_quant("v0")
+        nc.vector.tensor_reduce(out=ind[:], in_=idw[:].rearrange("p (m r) -> p r m", r=MOD), axis=AX.X, op=ALU.add)
+        sel = consts.tile([P, 4, W5, MOD + 1], F32)
+        nc.gpsimd.memset(sel[:], 0.0)
+        for j in range(W5):
+            nc.gpsimd.tensor_copy(
+                out=sel[:, :, j, j:MOD], in_=ind[:, 0 : MOD - j].unsqueeze(1).to_broadcast([P, 4, MOD - j])
+            )
+            if j > 0:
+                nc.gpsimd.tensor_copy(
+                    out=sel[:, :, j, 0:j], in_=ind[:, MOD - j : MOD].unsqueeze(1).to_broadcast([P, 4, j])
+                )
+        for tb, j, c in ((0, 0, 1), (0, 1, 0), (3, 3, NWIN - 1), (3, 4, NWIN - 2)):
+            nc.gpsimd.tensor_scalar(
+                out=sel[:, tb, j, MOD : MOD + 1], in0=band[:, c : c + 1], scalar1=BIG, scalar2=0.0, op0=ALU.mult, op1=ALU.add
+            )
         load_xp(PE_BATCHES[-1])
         load_k(PE_BATCHES[-1])
         for c in range(4, 8):
-            w_bank(c, "s")
+            w_bank(c, "sv"[c % 2])
         w_quant(1)
         qb = rawp.tile([P, NV, D], F32, tag="big")
         for vg in range(1, NV // 4):
@@ -392,41 +416,66 @@ def tile_crosssliceattention_pa_kernel(tc, x, Wq, bq, k_proj, out):
         for gi, b in enumerate(PE_BATCHES):
             nxt = PE_BATCHES[gi + 1] if gi + 1 < len(PE_BATCHES) else None
             nkey = "p%d" % nxt if nxt is not None else ""
-            sc_tile(b, 0)
+            front = new_scores()
+            score(b, 0, front, 0)
             if nxt is not None:
                 for j in range(3):
                     x_bank(nkey, j, "s")
-            vfill(2)
-            sc_tile(b, 1)
+            vfill(6)
+            score(b, 1, front, 1)
             if nxt is not None:
                 x_bank(nkey, 3, "s")
                 k_bank(nxt, 0, "s")
                 k_bank(nxt, 1, "s")
                 x_quant(nkey)
-            ex_half(b, 0)
-            vfill(2)
-            sc_tile(b, 2)
+            extract(b, 0, 2, front)
+            vfill(1)
+            back = new_scores()
+            score(b, 2, back, 0)
             if nxt is not None:
                 k_bank(nxt, 2, "s")
                 k_bank(nxt, 3, "s")
-            sc_tile(b, 3)
-            ex_half(b, 1)
-            if nxt is not None:
+                score(b, 3, back, 1)
+                extract(b, 2, 2, back)
                 for c in range(8):
                     mxp_group(nxt, c)
-                vfill(3)
+                vfill(2)
 
-        softmax(sc, 16, ypad[:, :, 0:16].rearrange("p j t -> p t j"), "p")
-
-        ta = tp.tile([P, 4, P], F32, tag="tp")
-        for j in range(4):
-            nc.tensor.transpose(ta[:, j, :], ypad[:, j, :], ident[:])
-        tb4 = tp.tile([P, 4, P], F32, tag="tp")
-        nc.tensor.transpose(tb4[:, 0, :], ypad[:, 4, :], ident[:])
-        z2 = small.tile([P, P, W5], F32)
-        nc.vector.tensor_copy(out=z2[:, :, 0:4], in_=ta[:].rearrange("s j p -> s p j"))
-        nc.vector.tensor_copy(out=z2[:, :, 4:5], in_=tb4[:, 0:1, :].rearrange("s j p -> s p j"))
-        ov = of.rearrange("(t p) j -> t (p j)", p=P)
+        final = PE_BATCHES[-1]
+        ready = 4 * final + 2
+        softmax(sc[:, 0:ready, :], ready, ypads["a"][:, :, 0:ready].rearrange("p j t -> p t j"), "p", ALU.min, -1.0)
+        extract(final, 2, 1, back)
+        lone = new_scores()
+        score(final, 3, lone, 0)
+        extract(final, 3, 1, lone)
+        low = small.tile([P, 2], F32)
+        nc.vector.tensor_reduce(out=low[:], in_=sc[:, ready : ready + 2, :], axis=AX.X, op=ALU.min)
+        exl = small.tile([P, 2, W5], F32)
+        sml = small.tile([P, 2], F32)
+        for i in range(2):
+            nc.scalar.activation(
+                out=exl[:, i, :],
+                in_=sc[:, ready + i, :],
+                func=ACT.Exp,
+                bias=low[:, i : i + 1],
+                scale=-1.0,
+                accum_out=sml[:, i : i + 1],
+            )
+        rsl = small.tile([P, 2], F32)
+        nc.vector.reciprocal(out=rsl[:], in_=sml[:])
+        nc.vector.tensor_tensor(
+            out=ypads["b"][:, :, 0:2].rearrange("p j t -> p t j"),
+            in0=exl[:],
+            in1=rsl[:].unsqueeze(2).to_broadcast([P, 2, W5]),
+            op=ALU.mult,
+        )
+        zja = turn("a")
+        za = small.tile([P, P, W5], F32)
+        nc.vector.tensor_copy(out=za[:], in_=zja[:].rearrange("s j p -> s p j"))
         for b in PE_BATCHES:
-            nc.sync.dma_start(out=ov[4 * b : 4 * b + 4, :], in_=z2[4 * b : 4 * b + 4, :, :].rearrange("s p j -> s (p j)"))
-        vfill(W5 * NV)
+            n = 4 if b != final else 2
+            nc.sync.dma_start(out=ov[4 * b : 4 * b + n, :], in_=za[4 * b : 4 * b + n, :, :].rearrange("s p j -> s (p j)"))
+        zjb = turn("b")
+        zb = small.tile([P, P, W5], F32)
+        nc.vector.tensor_copy(out=zb[:], in_=zjb[:].rearrange("s j p -> s p j"))
+        nc.sync.dma_start(out=ov[ready : ready + 2, :], in_=zb[0:2, :, :].rearrange("s p j -> s (p j)"))

@@ -183,12 +183,22 @@ def tile_crosssliceattention_pa_kernel(tc, x, Wq, bq, k_proj, out):
                     in_=gw[:, g, 2048 * h : 2048 * (h + 1)],
                 )
 
+        ordered = {}
+
+        def order(key, j, eng):
+            words = work.tile([P, 2, 2, P], F32, tag="order", bufs=4)
+            evac(eng, words[:], xraw[key][:].bitcast(F32)[:, j, :].rearrange("p (g w u) -> p g u w", g=2, u=2))
+            ordered[key, j] = words
+
         def x_bank(key, j, eng):
             if j == 0:
                 gt = gp.tile([P, 2, 4 * S], BF16, tag="g", align_bytes=64)
                 grp[key] = gt
             gf = grp[key][:].bitcast(F32).rearrange("p g (c u) -> p g c u", u=2)
-            bank = transpose_mx(xraw[key][:].bitcast(F32)[:, j, :])
+            if (key, j) in ordered:
+                bank = transpose_words(ordered[key, j][:].rearrange("p g u w -> p (g u w)"))
+            else:
+                bank = transpose_mx(xraw[key][:].bitcast(F32)[:, j, :])
             evac(eng, gf[:, :, P * j : P * (j + 1), :], bank[:].rearrange("p (g u) c -> p g c u", u=2))
 
         def x_quant(key):
@@ -397,6 +407,8 @@ def tile_crosssliceattention_pa_kernel(tc, x, Wq, bq, k_proj, out):
                 x_bank("v%d" % vg, j, "s")
             x_quant("v%d" % vg)
         first = PE_BATCHES[0]
+        for j in range(4):
+            order("p%d" % first, j, "s")
         for r in range(4):
             mxv_group(r, 0)
         for j in range(4):
@@ -417,6 +429,9 @@ def tile_crosssliceattention_pa_kernel(tc, x, Wq, bq, k_proj, out):
             nxt = PE_BATCHES[gi + 1] if gi + 1 < len(PE_BATCHES) else None
             nkey = "p%d" % nxt if nxt is not None else ""
             front = new_scores()
+            if nxt is not None:
+                for j in range(4):
+                    order(nkey, j, "s")
             score(b, 0, front, 0)
             if nxt is not None:
                 for j in range(3):

@@ -17,7 +17,7 @@ B, S, D = 4, 512, 1024
 W5 = 5
 NV = 4
 VS = 512
-PE_BATCHES = tuple([b for b in range(B) if not VS <= S * b < VS + P * NV])
+PE_BATCHES = (0, 2, 3)
 KPAD = 8
 KW = S + 2 * KPAD
 NWIN = 132
@@ -55,7 +55,11 @@ def tile_crosssliceattention_pa_kernel(tc, x, Wq, bq, k_proj, out):
         kraw = {}
 
         def load_w(u):
-            nc.sync.dma_start(out=w_raw[:, u, :, :], in_=wv[:, u, :, :])
+            if u == 0:
+                for e in range(2):
+                    nc.sync.dma_start(out=w_raw[:, u, e, :], in_=wv[:, u, e, :])
+            else:
+                nc.sync.dma_start(out=w_raw[:, u, :, :], in_=wv[:, u, :, :])
 
         def load_x(key, view):
             xr = rawp.tile([P, 4, D], BF16, tag="xr", bufs=3)
@@ -71,34 +75,35 @@ def tile_crosssliceattention_pa_kernel(tc, x, Wq, bq, k_proj, out):
             load_x("p%d" % b, xf[S * b : S * (b + 1), :].rearrange("(t p) i -> p t i", p=P))
 
         def load_k(b):
-            kr = rawp.tile([P, 4, D], BF16, name="kraw%d" % b)
+            kr = rawp.tile([P, 4, D], BF16, tag="kraw", bufs=3)
             view = kf[S * b : S * (b + 1), :].rearrange("(t p) d -> p t d", p=P)
             for hh in range(2):
                 nc.sync.dma_start(out=kr[:, 2 * hh : 2 * hh + 2, :], in_=view[:, 2 * hh : 2 * hh + 2, :])
             kraw[b] = kr
 
+        def load_kv():
+            base = VS - 2
+            nc.sync.dma_start(
+                out=k_v[:, 0:NV, :], in_=kf[base : base + P * NV, :].rearrange("(p c) d -> p c d", c=NV)
+            )
+            nc.sync.dma_start(
+                out=k_v[:, NV : 2 * NV, :],
+                in_=kf[base + NV : base + NV + P * NV, :].rearrange("(p c) d -> p c d", c=NV),
+            )
+
+        k_v = rawp.tile([P, 2 * NV, D], BF16)
+        first, second, third = PE_BATCHES
         load_w(0)
         load_w(1)
         nc.sync.dma_start(out=brow[0:4, :], in_=bq.rearrange("(u w) -> u w", u=4))
-        load_xv(0)
+        load_xp(first)
         load_w(2)
         load_w(3)
-        for vg in range(1, NV // 4):
-            load_xv(vg)
-        load_xp(PE_BATCHES[0])
-        load_k(PE_BATCHES[0])
-        k_v = rawp.tile([P, NV + 4, D], BF16)
-        base = VS - 2
-        nc.sync.dma_start(
-            out=k_v[:, 0:NV, :], in_=kf[base : base + P * NV, :].rearrange("(p c) d -> p c d", c=NV)
-        )
-        nc.sync.dma_start(
-            out=k_v[:, NV : NV + 4, :],
-            in_=kf[base + NV : base + NV + P * NV, :].rearrange("(p c) d -> p c d", c=NV)[:, 0:4, :],
-        )
-        for b in PE_BATCHES[1:-1]:
-            load_xp(b)
-            load_k(b)
+        load_xv(0)
+        load_k(first)
+        load_kv()
+        load_xp(second)
+        load_k(second)
 
         ident = consts.tile([P, P], F32)
         make_identity(nc, ident[:])
@@ -107,23 +112,38 @@ def tile_crosssliceattention_pa_kernel(tc, x, Wq, bq, k_proj, out):
         warm2 = consts.tile([P, 1], F32)
         nc.scalar.activation(out=warm2[:], in_=warm[:], func=ACT.Exp)
 
-        band = consts.tile([P, NWIN], F32)
-        nc.gpsimd.memset(band[:], 0.0)
-        for j in range(W5):
-            nc.gpsimd.tensor_tensor(out=band[:, j : j + P], in0=band[:, j : j + P], in1=ident[:], op=ALU.add)
         idw = consts.tile([P, NWIN], F32)
         nc.gpsimd.memset(idw[:], 0.0)
         nc.gpsimd.tensor_scalar(
             out=idw[:, 0:P], in0=ident[:], scalar1=-1.0 / 32.0, scalar2=0.0, op0=ALU.mult, op1=ALU.add
         )
         ind = consts.tile([P, MOD], F32)
+        nc.vector.tensor_reduce(out=ind[:], in_=idw[:].rearrange("p (m r) -> p r m", r=MOD), axis=AX.X, op=ALU.add)
+        band = consts.tile([P, NWIN], F32)
+        nc.gpsimd.memset(band[:], 0.0)
+        for j in range(W5):
+            nc.gpsimd.tensor_tensor(out=band[:, j : j + P], in0=band[:, j : j + P], in1=ident[:], op=ALU.add)
+        sel = consts.tile([P, 4, W5, MOD + 1], F32)
+        nc.gpsimd.memset(sel[:], 0.0)
+        for j in range(W5):
+            nc.gpsimd.tensor_copy(
+                out=sel[:, :, j, j:MOD], in_=ind[:, 0 : MOD - j].unsqueeze(1).to_broadcast([P, 4, MOD - j])
+            )
+            if j > 0:
+                nc.gpsimd.tensor_copy(
+                    out=sel[:, :, j, 0:j], in_=ind[:, MOD - j : MOD].unsqueeze(1).to_broadcast([P, 4, j])
+                )
+        for tb, j, c in ((0, 0, 1), (0, 1, 0), (3, 3, NWIN - 1), (3, 4, NWIN - 2)):
+            nc.gpsimd.tensor_scalar(
+                out=sel[:, tb, j, MOD : MOD + 1], in0=band[:, c : c + 1], scalar1=BIG, scalar2=0.0, op0=ALU.mult, op1=ALU.add
+            )
         negv = consts.tile([P, NV, W5], F32)
         nc.gpsimd.memset(negv[:], 0.0)
         for r, j0, j1, p in ((0, 0, 2, 0), (1, 0, 1, 0), (2, 4, 5, P - 1), (3, 3, 5, P - 1)):
             nc.gpsimd.tensor_scalar(
                 out=negv[:, r, j0:j1],
                 in0=ident[:, p : p + 1].to_broadcast([P, j1 - j0]),
-                scalar1=-BIG,
+                scalar1=BIG,
                 scalar2=0.0,
                 op0=ALU.mult,
                 op1=ALU.add,
@@ -132,7 +152,6 @@ def tile_crosssliceattention_pa_kernel(tc, x, Wq, bq, k_proj, out):
         nc.gpsimd.memset(rr[:], 0.0)
         nc.gpsimd.memset(rr[:, :, MOD : MOD + 1], 1.0)
         sc = small.tile([P, 16, W5], F32)
-        nc.gpsimd.memset(sc[:], 0.0)
         ypads = {}
         for part in ("a", "b"):
             yp = small.tile([P, W5, P], F32, name="ypad" + part)
@@ -223,7 +242,7 @@ def tile_crosssliceattention_pa_kernel(tc, x, Wq, bq, k_proj, out):
                 bank[:].bitcast(BF16).rearrange("p u (k e) -> p u e k", e=2),
             )
 
-        scv = small.tile([P, NV, W5], F32)
+        scv = sc[:, VS // P : VS // P + NV, :]
         vdone = [0]
 
         def mxv_group(r, h):
@@ -247,46 +266,42 @@ def tile_crosssliceattention_pa_kernel(tc, x, Wq, bq, k_proj, out):
                 op=ALU.add,
             )
 
-        def softmax(sc_t, groups, dest, label, extreme, scale):
-            mx = small.tile([P, groups], F32, name="mx" + label)
-            nc.vector.tensor_reduce(out=mx[:], in_=sc_t, axis=AX.X, op=extreme)
+        def softmax(sc_t, groups, dests, label):
+            mn = small.tile([P, groups], F32, name="mn" + label)
+            nc.vector.tensor_reduce(out=mn[:], in_=sc_t, axis=AX.X, op=ALU.min)
             nc.vector.tensor_tensor(
-                out=sc_t, in0=sc_t, in1=mx[:].unsqueeze(2).to_broadcast([P, groups, W5]), op=ALU.subtract
+                out=sc_t, in0=sc_t, in1=mn[:].unsqueeze(2).to_broadcast([P, groups, W5]), op=ALU.subtract
             )
             ex = small.tile([P, groups, W5], F32, name="ex" + label)
-            nc.scalar.activation(out=ex[:], in_=sc_t, func=ACT.Exp, scale=scale)
+            nc.scalar.activation(out=ex[:], in_=sc_t, func=ACT.Exp, scale=-1.0)
             sm = small.tile([P, groups], F32, name="sm" + label)
             nc.vector.tensor_reduce(out=sm[:], in_=ex[:], axis=AX.X, op=ALU.add)
             rs = small.tile([P, groups], F32, name="rs" + label)
             nc.vector.reciprocal(out=rs[:], in_=sm[:])
-            nc.vector.tensor_tensor(
-                out=dest, in0=ex[:], in1=rs[:].unsqueeze(2).to_broadcast([P, groups, W5]), op=ALU.mult
-            )
+            for g0, g1, dest in dests:
+                nc.vector.tensor_tensor(
+                    out=dest,
+                    in0=ex[:, g0:g1, :],
+                    in1=rs[:, g0:g1].unsqueeze(2).to_broadcast([P, g1 - g0, W5]),
+                    op=ALU.mult,
+                )
 
         def vfill(n):
             for i in range(n):
                 if vdone[0] >= W5 * NV:
                     return
                 r, j = divmod(vdone[0], W5)
-                junk = work.tile([P, D], F32, tag="junk", bufs=3)
+                junk = work.tile([P, D], F32, tag="junk", bufs=2)
                 nc.vector.scalar_tensor_tensor(
                     out=junk[:],
                     in0=qb[:, r, :],
-                    scalar=1.0,
+                    scalar=-1.0 / 32.0,
                     in1=k_v[:, r + j, :],
                     op0=ALU.mult,
                     op1=ALU.mult,
                     accum_out=scv[:, r, j : j + 1],
                 )
                 vdone[0] += 1
-                if vdone[0] == W5 * NV:
-                    nc.vector.tensor_tensor(out=scv[:], in0=scv[:], in1=negv[:], op=ALU.add)
-                    yv = small.tile([P, NV, W5], F32)
-                    softmax(scv[:], NV, yv[:], "v", ALU.max, 1.0 / 32.0)
-                    nc.sync.dma_start(
-                        out=of[VS : VS + P * NV, :].rearrange("(p r) j -> p (r j)", r=NV),
-                        in_=yv[:].rearrange("p r j -> p (r j)"),
-                    )
 
         def mxp_group(b, c):
             key = "p%d" % b
@@ -362,103 +377,104 @@ def tile_crosssliceattention_pa_kernel(tc, x, Wq, bq, k_proj, out):
             return zj
 
         for c in range(4):
-            w_bank(c, "sv"[c % 2])
+            w_bank(c, "svsv"[c])
         bt = tp.tile([P, 4, P], F32, tag="tp")
         nc.tensor.transpose(bt[:, 0, :], brow[:].bitcast(F32), ident[:])
         bw = consts.tile([P, 4], F32)
         nc.vector.tensor_copy(out=bw[:], in_=bt[:, 0, 0:4])
-        rep = consts.tile([P, 4, P], F32)
-        nc.vector.tensor_copy(out=rep[:], in_=bw[:].unsqueeze(2).to_broadcast([P, 4, P]))
         bpp = consts.tile([P, 8], F32)
         nc.vector.tensor_copy(out=bpp[:], in_=bw[:].bitcast(BF16))
-
         w_quant(0)
         for j in range(4):
-            x_bank("v0", j, "sv"[j % 2])
+            x_bank("p%d" % first, j, "svsv"[j])
+        rep = work.tile([P, 4, P], F32, tag="order", bufs=4)
+        nc.vector.tensor_copy(out=rep[:], in_=bw[:].unsqueeze(2).to_broadcast([P, 4, P]))
+        for c in range(4, 6):
+            w_bank(c, "ssss"[c - 4])
+        x_quant("p%d" % first)
+        for c in range(6, 8):
+            w_bank(c, "ssss"[c - 4])
+        qb = rawp.tile([P, NV, D], F32, tag="big")
+        for j in range(4):
+            order("v0", j, "vvvv"[j])
+        for c in range(4):
+            mxp_group(first, c)
+        w_quant(1)
         bbank = tp.tile([P, 4, P], F32, tag="tp")
         for u in range(4):
             nc.tensor.transpose(bbank[:, u, :], rep[:, u, :], ident[:])
+        for j in range(4):
+            x_bank("v0", j, "ssss"[j])
         bb = consts.tile([P, D], BF16)
         nc.vector.tensor_copy(out=bb[:].bitcast(F32), in_=bbank[:].rearrange("p u w -> p (u w)"))
         x_quant("v0")
-        nc.vector.tensor_reduce(out=ind[:], in_=idw[:].rearrange("p (m r) -> p r m", r=MOD), axis=AX.X, op=ALU.add)
-        sel = consts.tile([P, 4, W5, MOD + 1], F32)
-        nc.gpsimd.memset(sel[:], 0.0)
-        for j in range(W5):
-            nc.gpsimd.tensor_copy(
-                out=sel[:, :, j, j:MOD], in_=ind[:, 0 : MOD - j].unsqueeze(1).to_broadcast([P, 4, MOD - j])
-            )
-            if j > 0:
-                nc.gpsimd.tensor_copy(
-                    out=sel[:, :, j, 0:j], in_=ind[:, MOD - j : MOD].unsqueeze(1).to_broadcast([P, 4, j])
-                )
-        for tb, j, c in ((0, 0, 1), (0, 1, 0), (3, 3, NWIN - 1), (3, 4, NWIN - 2)):
-            nc.gpsimd.tensor_scalar(
-                out=sel[:, tb, j, MOD : MOD + 1], in0=band[:, c : c + 1], scalar1=BIG, scalar2=0.0, op0=ALU.mult, op1=ALU.add
-            )
-        load_xp(PE_BATCHES[-1])
-        load_k(PE_BATCHES[-1])
+        for tb in range(0):
+            k_bank(first, tb, "svsv"[tb])
         for c in range(4, 8):
-            w_bank(c, "sv"[c % 2])
-        w_quant(1)
-        qb = rawp.tile([P, NV, D], F32, tag="big")
-        for vg in range(1, NV // 4):
-            for j in range(4):
-                x_bank("v%d" % vg, j, "s")
-            x_quant("v%d" % vg)
-        first = PE_BATCHES[0]
-        for j in range(4):
-            order("p%d" % first, j, "s")
-        for r in range(4):
-            mxv_group(r, 0)
-        for j in range(4):
-            x_bank("p%d" % first, j, "s")
-        x_quant("p%d" % first)
-        for tb in range(4):
-            k_bank(first, tb, "s")
-        for r in range(4):
-            mxv_group(r, 1)
-        for r in range(4, NV):
-            mxv_group(r, 0)
-            mxv_group(r, 1)
-        for c in range(8):
             mxp_group(first, c)
-        vfill(3)
+        load_xp(third)
+        for tb in range(0, 4):
+            k_bank(first, tb, "svsv"[tb])
+        load_k(third)
+        for r in range(4):
+            for h in range(2):
+                mxv_group(r, h)
+            vfill(0 if r > 1 else 0)
 
-        for gi, b in enumerate(PE_BATCHES):
-            nxt = PE_BATCHES[gi + 1] if gi + 1 < len(PE_BATCHES) else None
-            nkey = "p%d" % nxt if nxt is not None else ""
+        for b, nxt in ((first, second), (second, third), (third, None)):
             front = new_scores()
-            if nxt is not None:
-                for j in range(4):
-                    order(nkey, j, "s")
             score(b, 0, front, 0)
             if nxt is not None:
-                for j in range(3):
-                    x_bank(nkey, j, "s")
-            vfill(6)
-            score(b, 1, front, 1)
-            if nxt is not None:
-                x_bank(nkey, 3, "s")
-                k_bank(nxt, 0, "s")
-                k_bank(nxt, 1, "s")
-                x_quant(nkey)
-            extract(b, 0, 2, front)
-            vfill(1)
-            back = new_scores()
-            score(b, 2, back, 0)
-            if nxt is not None:
-                k_bank(nxt, 2, "s")
-                k_bank(nxt, 3, "s")
-                score(b, 3, back, 1)
-                extract(b, 2, 2, back)
-                for c in range(8):
-                    mxp_group(nxt, c)
+                for j in range(4):
+                    order("p%d" % nxt, j, "ssss"[j])
+                for j in range(2):
+                    x_bank("p%d" % nxt, j, "s")
                 vfill(2)
+            score(b, 1, front, 1)
+            if nxt is None:
+                vfill(W5 * NV)
+            if nxt is not None:
+                for j in range(2, 4):
+                    x_bank("p%d" % nxt, j, "s")
+                vfill(2)
+                k_bank(nxt, 0, "s")
+            extract(b, 0, 2, front)
+            back = new_scores()
+            if nxt is not None:
+                x_quant("p%d" % nxt)
+                vfill(1)
+                score(b, 2, back, 0)
+                for tb in range(1, 4):
+                    k_bank(nxt, tb, "s")
+                for c in range(4):
+                    mxp_group(nxt, c)
+                score(b, 3, back, 1)
+                for c in range(4, 8):
+                    mxp_group(nxt, c)
+                vfill(4)
+                extract(b, 2, 2, back)
+                vfill(1)
 
-        final = PE_BATCHES[-1]
+        final = third
+        score(final, 2, back, 0)
+        vfill(W5 * NV)
+        nc.vector.tensor_tensor(out=scv, in0=scv, in1=negv[:], op=ALU.add)
         ready = 4 * final + 2
-        softmax(sc[:, 0:ready, :], ready, ypads["a"][:, :, 0:ready].rearrange("p j t -> p t j"), "p", ALU.min, -1.0)
+        yv = small.tile([P, NV, W5], F32)
+        ya = ypads["a"]
+        softmax(
+            sc[:, 0:ready, :],
+            ready,
+            (
+                (0, 4, ya[:, :, 0:4].rearrange("p j t -> p t j")),
+                (8, ready, ya[:, :, 8:ready].rearrange("p j t -> p t j")),
+                (4, 8, yv[:]),
+            ),
+            "p",
+        )
+        nc.sync.dma_start(
+            out=of[VS : VS + P * NV, :].rearrange("(p r) j -> p (r j)", r=NV), in_=yv[:].rearrange("p r j -> p (r j)")
+        )
         extract(final, 2, 1, back)
         lone = new_scores()
         score(final, 3, lone, 0)

@@ -1,7 +1,6 @@
 from contextlib import ExitStack
 
 import concourse.mybir as mybir
-from concourse.masks import make_identity
 
 F32 = mybir.dt.float32
 BF16 = mybir.dt.bfloat16
@@ -105,58 +104,54 @@ def tile_crosssliceattention_pa_kernel(tc, x, Wq, bq, k_proj, out):
         load_xp(second)
         load_k(second)
 
-        ident = consts.tile([P, P], F32)
-        make_identity(nc, ident[:])
+        ramp = consts.tile([P, NWIN], F32)
+        nc.gpsimd.iota(ramp[:], pattern=[[1, NWIN]], base=0, channel_multiplier=-1, allow_small_or_imprecise_dtypes=True)
         warm = consts.tile([P, 1], F32)
-        nc.gpsimd.memset(warm[:], 0.0)
+        nc.vector.memset(warm[:], 0.0)
         warm2 = consts.tile([P, 1], F32)
         nc.scalar.activation(out=warm2[:], in_=warm[:], func=ACT.Exp)
-
-        idw = consts.tile([P, NWIN], F32)
-        nc.gpsimd.memset(idw[:], 0.0)
-        nc.gpsimd.tensor_scalar(
-            out=idw[:, 0:P], in0=ident[:], scalar1=-1.0 / 32.0, scalar2=0.0, op0=ALU.mult, op1=ALU.add
+        unit = consts.tile([P, NWIN], F32)
+        nc.vector.tensor_scalar(out=unit[:], in0=ramp[:], scalar1=0.0, scalar2=None, op0=ALU.is_equal)
+        ident = unit[:, 0:P]
+        ahead = consts.tile([P, NWIN], F32)
+        nc.vector.tensor_scalar(out=ahead[:], in0=ramp[:], scalar1=0.0, scalar2=None, op0=ALU.is_ge)
+        band = consts.tile([P, NWIN], F32)
+        nc.vector.scalar_tensor_tensor(
+            out=band[:], in0=ramp[:], scalar=float(W5 - 1), in1=ahead[:], op0=ALU.is_le, op1=ALU.mult
         )
         ind = consts.tile([P, MOD], F32)
-        nc.vector.tensor_reduce(out=ind[:], in_=idw[:].rearrange("p (m r) -> p r m", r=MOD), axis=AX.X, op=ALU.add)
-        band = consts.tile([P, NWIN], F32)
-        nc.gpsimd.memset(band[:], 0.0)
-        for j in range(W5):
-            nc.gpsimd.tensor_tensor(out=band[:, j : j + P], in0=band[:, j : j + P], in1=ident[:], op=ALU.add)
+        nc.vector.tensor_reduce(out=ind[:], in_=unit[:].rearrange("p (m r) -> p r m", r=MOD), axis=AX.X, op=ALU.add)
         sel = consts.tile([P, 4, W5, MOD + 1], F32)
-        nc.gpsimd.memset(sel[:], 0.0)
-        for j in range(W5):
-            nc.gpsimd.tensor_copy(
-                out=sel[:, :, j, j:MOD], in_=ind[:, 0 : MOD - j].unsqueeze(1).to_broadcast([P, 4, MOD - j])
-            )
-            if j > 0:
-                nc.gpsimd.tensor_copy(
-                    out=sel[:, :, j, 0:j], in_=ind[:, MOD - j : MOD].unsqueeze(1).to_broadcast([P, 4, j])
-                )
-        for tb, j, c in ((0, 0, 1), (0, 1, 0), (3, 3, NWIN - 1), (3, 4, NWIN - 2)):
-            nc.gpsimd.tensor_scalar(
-                out=sel[:, tb, j, MOD : MOD + 1], in0=band[:, c : c + 1], scalar1=BIG, scalar2=0.0, op0=ALU.mult, op1=ALU.add
-            )
+        nc.vector.memset(sel[:], 0.0)
         negv = consts.tile([P, NV, W5], F32)
-        nc.gpsimd.memset(negv[:], 0.0)
-        for r, j0, j1, p in ((0, 0, 2, 0), (1, 0, 1, 0), (2, 4, 5, P - 1), (3, 3, 5, P - 1)):
-            nc.gpsimd.tensor_scalar(
-                out=negv[:, r, j0:j1],
-                in0=ident[:, p : p + 1].to_broadcast([P, j1 - j0]),
-                scalar1=BIG,
-                scalar2=0.0,
-                op0=ALU.mult,
-                op1=ALU.add,
-            )
+        nc.vector.memset(negv[:], 0.0)
         rr = small.tile([P, 16, MOD + 1], F32)
-        nc.gpsimd.memset(rr[:], 0.0)
-        nc.gpsimd.memset(rr[:, :, MOD : MOD + 1], 1.0)
+        nc.vector.memset(rr[:], 1.0)
         sc = small.tile([P, 16, W5], F32)
         ypads = {}
         for part in ("a", "b"):
             yp = small.tile([P, W5, P], F32, name="ypad" + part)
-            nc.gpsimd.memset(yp[:], 0.0)
+            nc.vector.memset(yp[:], 0.0)
             ypads[part] = yp
+
+        def masks():
+            ind2 = consts.tile([P, 2, MOD], F32)
+            nc.scalar.activation(
+                out=ind2[:], in_=ind[:].unsqueeze(1).to_broadcast([P, 2, MOD]), func=ACT.Copy, scale=-1.0 / 32.0
+            )
+            twice = ind2[:].rearrange("p a r -> p (a r)")
+            for j in range(W5):
+                nc.scalar.copy(
+                    out=sel[:, :, j, 0:MOD], in_=twice[:, MOD - j : 2 * MOD - j].unsqueeze(1).to_broadcast([P, 4, MOD])
+                )
+            for tb, j, c in ((0, 0, 1), (0, 1, 0), (3, 3, NWIN - 1), (3, 4, NWIN - 2)):
+                nc.scalar.activation(
+                    out=sel[:, tb, j, MOD : MOD + 1], in_=band[:, c : c + 1], func=ACT.Copy, scale=BIG
+                )
+            for r, j0, j1, p in ((0, 0, 2, 0), (1, 0, 1, 0), (2, 4, 5, P - 1), (3, 3, 5, P - 1)):
+                nc.scalar.activation(
+                    out=negv[:, r, j0:j1], in_=unit[:, p : p + 1].to_broadcast([P, j1 - j0]), func=ACT.Copy, scale=BIG
+                )
 
         def evac(eng, out_ap, in_ap):
             if eng == "v":
@@ -167,7 +162,7 @@ def tile_crosssliceattention_pa_kernel(tc, x, Wq, bq, k_proj, out):
         def transpose_words(words):
             bank = tp.tile([P, 4, P], F32, tag="tp")
             for blk in range(4):
-                nc.tensor.transpose(bank[:, blk, :], words[:, P * blk : P * (blk + 1)], ident[:])
+                nc.tensor.transpose(bank[:, blk, :], words[:, P * blk : P * (blk + 1)], ident)
             return bank
 
         def transpose_mx(words):
@@ -175,7 +170,7 @@ def tile_crosssliceattention_pa_kernel(tc, x, Wq, bq, k_proj, out):
             for g in range(2):
                 for u in range(2):
                     nc.tensor.transpose(
-                        bank[:, 2 * g + u, :], words[:, 2 * P * g + u : 2 * P * (g + 1) : 2], ident[:]
+                        bank[:, 2 * g + u, :], words[:, 2 * P * g + u : 2 * P * (g + 1) : 2], ident
                     )
             return bank
 
@@ -367,7 +362,7 @@ def tile_crosssliceattention_pa_kernel(tc, x, Wq, bq, k_proj, out):
             ta = tp.tile([P, 4, P], F32, tag="tp")
             tb2 = tp.tile([P, 4, P], F32, tag="tp")
             for j in range(W5):
-                nc.tensor.transpose(ta[:, j, :] if j < 3 else tb2[:, j - 3, :], yp[:, j, :], ident[:])
+                nc.tensor.transpose(ta[:, j, :] if j < 3 else tb2[:, j - 3, :], yp[:, j, :], ident)
             zj = small.tile([P, W5, P], F32, name="zj" + part)
             nc.scalar.copy(out=zj[:, 3:5, :], in_=tb2[:, 0:2, :])
             if part == "a":
@@ -379,7 +374,7 @@ def tile_crosssliceattention_pa_kernel(tc, x, Wq, bq, k_proj, out):
         for c in range(4):
             w_bank(c, "svsv"[c])
         bt = tp.tile([P, 4, P], F32, tag="tp")
-        nc.tensor.transpose(bt[:, 0, :], brow[:].bitcast(F32), ident[:])
+        nc.tensor.transpose(bt[:, 0, :], brow[:].bitcast(F32), ident)
         bw = consts.tile([P, 4], F32)
         nc.vector.tensor_copy(out=bw[:], in_=bt[:, 0, 0:4])
         bpp = consts.tile([P, 8], F32)
@@ -402,31 +397,30 @@ def tile_crosssliceattention_pa_kernel(tc, x, Wq, bq, k_proj, out):
         w_quant(1)
         bbank = tp.tile([P, 4, P], F32, tag="tp")
         for u in range(4):
-            nc.tensor.transpose(bbank[:, u, :], rep[:, u, :], ident[:])
+            nc.tensor.transpose(bbank[:, u, :], rep[:, u, :], ident)
         for j in range(4):
             x_bank("v0", j, "ssss"[j])
         bb = consts.tile([P, D], BF16)
         nc.vector.tensor_copy(out=bb[:].bitcast(F32), in_=bbank[:].rearrange("p u w -> p (u w)"))
         x_quant("v0")
-        for tb in range(0):
-            k_bank(first, tb, "svsv"[tb])
         for c in range(4, 8):
             mxp_group(first, c)
         load_xp(third)
-        for tb in range(0, 4):
+        for tb in range(4):
             k_bank(first, tb, "svsv"[tb])
         load_k(third)
         for r in range(4):
             for h in range(2):
                 mxv_group(r, h)
-            vfill(0 if r > 1 else 0)
 
         for b, nxt in ((first, second), (second, third), (third, None)):
             front = new_scores()
             score(b, 0, front, 0)
             if nxt is not None:
                 for j in range(4):
-                    order("p%d" % nxt, j, "ssss"[j])
+                    order("p%d" % nxt, j, "s")
+                if b == first:
+                    masks()
                 for j in range(2):
                     x_bank("p%d" % nxt, j, "s")
                 vfill(2)

@@ -218,10 +218,15 @@ def tile_crosssliceattention_pa_kernel(tc, x, Wq, bq, k_proj, out):
         def x_quant(key):
             xcb = codes.tile([P, 2, S], U32, name="xc" + key, align_bytes=64)
             xsb = codes.tile([P, 2, S], U8, name="xs" + key, align_bytes=64)
-            for g in range(2):
-                nc.vector.quantize_mx(out=xcb[:, g, :].bitcast(FP8X4), scales=xsb[:, g, :], in_=grp[key][:, g, :])
             xc[key] = xcb
             xs[key] = xsb
+
+            def part(g):
+                return lambda: nc.vector.quantize_mx(
+                    out=xcb[:, g, :].bitcast(FP8X4), scales=xsb[:, g, :], in_=grp[key][:, g, :]
+                )
+
+            return [part(0), part(1)]
 
         def k_bank(b, tb, eng):
             if tb == 0:
@@ -263,23 +268,32 @@ def tile_crosssliceattention_pa_kernel(tc, x, Wq, bq, k_proj, out):
 
         def softmax(sc_t, groups, dests, label):
             mn = small.tile([P, groups], F32, name="mn" + label)
-            nc.vector.tensor_reduce(out=mn[:], in_=sc_t, axis=AX.X, op=ALU.min)
-            nc.vector.tensor_tensor(
-                out=sc_t, in0=sc_t, in1=mn[:].unsqueeze(2).to_broadcast([P, groups, W5]), op=ALU.subtract
-            )
             ex = small.tile([P, groups, W5], F32, name="ex" + label)
-            nc.scalar.activation(out=ex[:], in_=sc_t, func=ACT.Exp, scale=-1.0)
             sm = small.tile([P, groups], F32, name="sm" + label)
-            nc.vector.tensor_reduce(out=sm[:], in_=ex[:], axis=AX.X, op=ALU.add)
             rs = small.tile([P, groups], F32, name="rs" + label)
-            nc.vector.reciprocal(out=rs[:], in_=sm[:])
-            for g0, g1, dest in dests:
+
+            def shift():
                 nc.vector.tensor_tensor(
-                    out=dest,
-                    in0=ex[:, g0:g1, :],
-                    in1=rs[:, g0:g1].unsqueeze(2).to_broadcast([P, g1 - g0, W5]),
-                    op=ALU.mult,
+                    out=sc_t, in0=sc_t, in1=mn[:].unsqueeze(2).to_broadcast([P, groups, W5]), op=ALU.subtract
                 )
+                nc.scalar.activation(out=ex[:], in_=sc_t, func=ACT.Exp, scale=-1.0)
+
+            def scale():
+                for g0, g1, dest in dests:
+                    nc.vector.tensor_tensor(
+                        out=dest,
+                        in0=ex[:, g0:g1, :],
+                        in1=rs[:, g0:g1].unsqueeze(2).to_broadcast([P, g1 - g0, W5]),
+                        op=ALU.mult,
+                    )
+
+            return [
+                lambda: nc.vector.tensor_reduce(out=mn[:], in_=sc_t, axis=AX.X, op=ALU.min),
+                shift,
+                lambda: nc.vector.tensor_reduce(out=sm[:], in_=ex[:], axis=AX.X, op=ALU.add),
+                lambda: nc.vector.reciprocal(out=rs[:], in_=sm[:]),
+                scale,
+            ]
 
         def vfill(n):
             for i in range(n):
@@ -332,28 +346,43 @@ def tile_crosssliceattention_pa_kernel(tc, x, Wq, bq, k_proj, out):
                 )
 
         def extract(b, tb, n, sps):
-            bm = work.tile([P, 2, NWIN], F32, tag="bm")
-            nc.vector.tensor_tensor(
-                out=bm[:, 0:n, :],
-                in0=sps[:, 0:n, :],
-                in1=band[:].unsqueeze(1).to_broadcast([P, n, NWIN]),
-                op=ALU.mult,
-            )
             slot = 4 * b + tb
-            nc.vector.tensor_reduce(
-                out=rr[:, slot : slot + n, 0:MOD],
-                in_=bm[:, 0:n, :].rearrange("p t (m r) -> p t r m", r=MOD),
-                axis=AX.X,
-                op=ALU.add,
-            )
+            bm = work.tile([P, 2, NWIN], F32, tag="bm")
             pr = work.tile([P, 2, W5, MOD + 1], F32, tag="pr")
-            nc.vector.tensor_tensor(
-                out=pr[:, 0:n, :, :],
-                in0=rr[:, slot : slot + n, :].unsqueeze(2).to_broadcast([P, n, W5, MOD + 1]),
-                in1=sel[:, tb : tb + n, :, :],
-                op=ALU.mult,
-            )
-            nc.vector.tensor_reduce(out=sc[:, slot : slot + n, :], in_=pr[:, 0:n, :, :], axis=AX.X, op=ALU.add)
+            return [
+                lambda: nc.vector.tensor_tensor(
+                    out=bm[:, 0:n, :],
+                    in0=sps[:, 0:n, :],
+                    in1=band[:].unsqueeze(1).to_broadcast([P, n, NWIN]),
+                    op=ALU.mult,
+                ),
+                lambda: nc.vector.tensor_reduce(
+                    out=rr[:, slot : slot + n, 0:MOD],
+                    in_=bm[:, 0:n, :].rearrange("p t (m r) -> p t r m", r=MOD),
+                    axis=AX.X,
+                    op=ALU.add,
+                ),
+                lambda: nc.vector.tensor_tensor(
+                    out=pr[:, 0:n, :, :],
+                    in0=rr[:, slot : slot + n, :].unsqueeze(2).to_broadcast([P, n, W5, MOD + 1]),
+                    in1=sel[:, tb : tb + n, :, :],
+                    op=ALU.mult,
+                ),
+                lambda: nc.vector.tensor_reduce(
+                    out=sc[:, slot : slot + n, :], in_=pr[:, 0:n, :, :], axis=AX.X, op=ALU.add
+                ),
+            ]
+
+        def weave(steps, others=()):
+            others = list(others)
+            for i, step in enumerate(steps):
+                step()
+                if i < len(others):
+                    others[i]()
+                elif i + 1 < len(steps):
+                    vfill(1)
+            for other in others[len(steps):]:
+                other()
 
         ov = of.rearrange("(t p) j -> t (p j)", p=P)
 
@@ -386,7 +415,8 @@ def tile_crosssliceattention_pa_kernel(tc, x, Wq, bq, k_proj, out):
         nc.vector.tensor_copy(out=rep[:], in_=bw[:].unsqueeze(2).to_broadcast([P, 4, P]))
         for c in range(4, 6):
             w_bank(c, "ssss"[c - 4])
-        x_quant("p%d" % first)
+        for step in x_quant("p%d" % first):
+            step()
         for c in range(6, 8):
             w_bank(c, "ssss"[c - 4])
         qb = rawp.tile([P, NV, D], F32, tag="big")
@@ -402,7 +432,8 @@ def tile_crosssliceattention_pa_kernel(tc, x, Wq, bq, k_proj, out):
             x_bank("v0", j, "ssss"[j])
         bb = consts.tile([P, D], BF16)
         nc.vector.tensor_copy(out=bb[:].bitcast(F32), in_=bbank[:].rearrange("p u w -> p (u w)"))
-        x_quant("v0")
+        for step in x_quant("v0"):
+            step()
         for c in range(4, 8):
             mxp_group(first, c)
         load_xp(third)
@@ -430,12 +461,15 @@ def tile_crosssliceattention_pa_kernel(tc, x, Wq, bq, k_proj, out):
             if nxt is not None:
                 for j in range(2, 4):
                     x_bank("p%d" % nxt, j, "s")
-                vfill(2)
+                vfill(1)
                 k_bank(nxt, 0, "s")
-            extract(b, 0, 2, front)
+            steps = extract(b, 0, 2, front)
+            if nxt is not None:
+                weave(steps, [lambda: vfill(1)] + x_quant("p%d" % nxt))
+            else:
+                weave(steps)
             back = new_scores()
             if nxt is not None:
-                x_quant("p%d" % nxt)
                 vfill(1)
                 score(b, 2, back, 0)
                 for tb in range(1, 4):
@@ -445,9 +479,9 @@ def tile_crosssliceattention_pa_kernel(tc, x, Wq, bq, k_proj, out):
                 score(b, 3, back, 1)
                 for c in range(4, 8):
                     mxp_group(nxt, c)
-                vfill(4)
-                extract(b, 2, 2, back)
-                vfill(1)
+                vfill(2)
+                weave(extract(b, 2, 2, back))
+                vfill(0)
 
         final = third
         score(final, 2, back, 0)
@@ -456,7 +490,7 @@ def tile_crosssliceattention_pa_kernel(tc, x, Wq, bq, k_proj, out):
         ready = 4 * final + 2
         yv = small.tile([P, NV, W5], F32)
         ya = ypads["a"]
-        softmax(
+        early = softmax(
             sc[:, 0:ready, :],
             ready,
             (
@@ -466,13 +500,13 @@ def tile_crosssliceattention_pa_kernel(tc, x, Wq, bq, k_proj, out):
             ),
             "p",
         )
+        weave(early, extract(final, 2, 1, back))
         nc.sync.dma_start(
             out=of[VS : VS + P * NV, :].rearrange("(p r) j -> p (r j)", r=NV), in_=yv[:].rearrange("p r j -> p (r j)")
         )
-        extract(final, 2, 1, back)
         lone = new_scores()
         score(final, 3, lone, 0)
-        extract(final, 3, 1, lone)
+        weave(extract(final, 3, 1, lone))
         low = small.tile([P, 2], F32)
         nc.vector.tensor_reduce(out=low[:], in_=sc[:, ready : ready + 2, :], axis=AX.X, op=ALU.min)
         exl = small.tile([P, 2, W5], F32)

from contextlib import ExitStack

import concourse.mybir as mybir

F32 = mybir.dt.float32
BF16 = mybir.dt.bfloat16
U32 = mybir.dt.uint32
U8 = mybir.dt.uint8
FP8X4 = mybir.dt.float8_e4m3fn_x4
ALU = mybir.AluOpType
ACT = mybir.ActivationFunctionType
AX = mybir.AxisListType

P = 128
B, S, D = 4, 512, 1024
W5 = 5
NV = 4
VS = 512
PE_BATCHES = (0, 2, 3)
KPAD = 8
KW = S + 2 * KPAD
NWIN = 132
MOD = 6
BIG = 1.0e30

FLOPS = 2 * B * S * D * D + 2 * B * S * W5 * D


def tile_crosssliceattention_pa_kernel(tc, x, Wq, bq, k_proj, out):
    nc = tc.nc
    xf = x.flatten_outer_dims()
    kf = k_proj.flatten_outer_dims()
    of = out.flatten_outer_dims()

    with ExitStack() as ctx:
        consts = ctx.enter_context(tc.tile_pool(name="consts", bufs=1))
        rawp = ctx.enter_context(tc.tile_pool(name="raw", bufs=1))
        gp = ctx.enter_context(tc.tile_pool(name="grouped", bufs=2))
        ktp = ctx.enter_context(tc.tile_pool(name="kt", bufs=2))
        qtp = ctx.enter_context(tc.tile_pool(name="qt", bufs=2))
        codes = ctx.enter_context(tc.tile_pool(name="codes", bufs=1))
        work = ctx.enter_context(tc.tile_pool(name="work", bufs=2))
        small = ctx.enter_context(tc.tile_pool(name="small", bufs=1))
        tp = ctx.enter_context(tc.psum_pool(name="banks", bufs=6))
        sp = ctx.enter_context(tc.psum_pool(name="sps", bufs=2))
        ctx.enter_context(tc.manual_schedule())

        brow = consts.tile([P, 2 * P], BF16)
        nc.vector.memset(brow[:], 0.0)

        w_raw = rawp.tile([P, 4, 2, D], BF16, tag="big")
        wv = Wq.rearrange("(u p e) i -> p u e i", p=P, e=2)
        xraw = {}
        kraw = {}

        def load_w(u):
            if u == 0:
                for e in range(2):
                    nc.sync.dma_start(out=w_raw[:, u, e, :], in_=wv[:, u, e, :])
            else:
                nc.sync.dma_start(out=w_raw[:, u, :, :], in_=wv[:, u, :, :])

        def load_x(key, view):
            xr = rawp.tile([P, 4, D], BF16, tag="xr", bufs=3)
            for hh in range(2):
                nc.sync.dma_start(out=xr[:, 2 * hh : 2 * hh + 2, :], in_=view[:, 2 * hh : 2 * hh + 2, :])
            xraw[key] = xr

        def load_xv(vg):
            view = xf[VS : VS + P * NV, :].rearrange("(p r) i -> p r i", r=NV)
            load_x("v%d" % vg, view[:, 4 * vg : 4 * vg + 4, :])

        def load_xp(b):
            load_x("p%d" % b, xf[S * b : S * (b + 1), :].rearrange("(t p) i -> p t i", p=P))

        def load_k(b):
            kr = rawp.tile([P, 4, D], BF16, tag="kraw", bufs=3)
            view = kf[S * b : S * (b + 1), :].rearrange("(t p) d -> p t d", p=P)
            for hh in range(2):
                nc.sync.dma_start(out=kr[:, 2 * hh : 2 * hh + 2, :], in_=view[:, 2 * hh : 2 * hh + 2, :])
            kraw[b] = kr

        def load_kv():
            base = VS - 2
            nc.sync.dma_start(
                out=k_v[:, 0:NV, :], in_=kf[base : base + P * NV, :].rearrange("(p c) d -> p c d", c=NV)
            )
            nc.sync.dma_start(
                out=k_v[:, NV : 2 * NV, :],
                in_=kf[base + NV : base + NV + P * NV, :].rearrange("(p c) d -> p c d", c=NV),
            )

        k_v = rawp.tile([P, 2 * NV, D], BF16)
        first, second, third = PE_BATCHES
        load_w(0)
        load_w(1)
        nc.sync.dma_start(out=brow[0:4, :], in_=bq.rearrange("(u w) -> u w", u=4))
        load_xp(first)
        load_w(2)
        load_w(3)
        load_xv(0)
        load_k(first)
        load_kv()
        load_xp(second)
        load_k(second)

        ramp = consts.tile([P, NWIN], F32)
        nc.gpsimd.iota(ramp[:], pattern=[[1, NWIN]], base=0, channel_multiplier=-1, allow_small_or_imprecise_dtypes=True)
        warm = consts.tile([P, 1], F32)
        nc.vector.memset(warm[:], 0.0)
        warm2 = consts.tile([P, 1], F32)
        nc.scalar.activation(out=warm2[:], in_=warm[:], func=ACT.Exp)
        unit = consts.tile([P, NWIN], F32)
        nc.vector.tensor_scalar(out=unit[:], in0=ramp[:], scalar1=0.0, scalar2=None, op0=ALU.is_equal)
        ident = unit[:, 0:P]
        ahead = consts.tile([P, NWIN], F32)
        nc.vector.tensor_scalar(out=ahead[:], in0=ramp[:], scalar1=0.0, scalar2=None, op0=ALU.is_ge)
        band = consts.tile([P, NWIN], F32)
        nc.vector.scalar_tensor_tensor(
            out=band[:], in0=ramp[:], scalar=float(W5 - 1), in1=ahead[:], op0=ALU.is_le, op1=ALU.mult
        )
        ind = consts.tile([P, MOD], F32)
        nc.vector.tensor_reduce(out=ind[:], in_=unit[:].rearrange("p (m r) -> p r m", r=MOD), axis=AX.X, op=ALU.add)
        sel = consts.tile([P, 4, W5, MOD + 1], F32)
        nc.vector.memset(sel[:], 0.0)
        negv = consts.tile([P, NV, W5], F32)
        nc.vector.memset(negv[:], 0.0)
        rr = small.tile([P, 16, MOD + 1], F32)
        nc.vector.memset(rr[:], 1.0)
        sc = small.tile([P, 16, W5], F32)
        ypads = {}
        for part in ("a", "b"):
            yp = small.tile([P, W5, P], F32, name="ypad" + part)
            nc.vector.memset(yp[:], 0.0)
            ypads[part] = yp

        def masks():
            ind2 = consts.tile([P, 2, MOD], F32)
            nc.scalar.activation(
                out=ind2[:], in_=ind[:].unsqueeze(1).to_broadcast([P, 2, MOD]), func=ACT.Copy, scale=-1.0 / 32.0
            )
            twice = ind2[:].rearrange("p a r -> p (a r)")
            for j in range(W5):
                nc.scalar.copy(
                    out=sel[:, :, j, 0:MOD], in_=twice[:, MOD - j : 2 * MOD - j].unsqueeze(1).to_broadcast([P, 4, MOD])
                )
            for tb, j, c in ((0, 0, 1), (0, 1, 0), (3, 3, NWIN - 1), (3, 4, NWIN - 2)):
                nc.scalar.activation(
                    out=sel[:, tb, j, MOD : MOD + 1], in_=band[:, c : c + 1], func=ACT.Copy, scale=BIG
                )
            for r, j0, j1, p in ((0, 0, 2, 0), (1, 0, 1, 0), (2, 4, 5, P - 1), (3, 3, 5, P - 1)):
                nc.scalar.activation(
                    out=negv[:, r, j0:j1], in_=unit[:, p : p + 1].to_broadcast([P, j1 - j0]), func=ACT.Copy, scale=BIG
                )

        def evac(eng, out_ap, in_ap):
            if eng == "v":
                nc.vector.tensor_copy(out=out_ap, in_=in_ap)
            else:
                nc.scalar.copy(out=out_ap, in_=in_ap)

        def transpose_words(words):
            bank = tp.tile([P, 4, P], F32, tag="tp")
            for blk in range(4):
                nc.tensor.transpose(bank[:, blk, :], words[:, P * blk : P * (blk + 1)], ident)
            return bank

        def transpose_mx(words):
            bank = tp.tile([P, 4, P], F32, tag="tp")
            for g in range(2):
                for u in range(2):
                    nc.tensor.transpose(
                        bank[:, 2 * g + u, :], words[:, 2 * P * g + u : 2 * P * (g + 1) : 2], ident
                    )
            return bank

        wc = codes.tile([P, 2, D], U32, align_bytes=64)
        ws = codes.tile([P, 2, D], U8, align_bytes=64)
        gw = ktp.tile([P, 2, 4 * D], BF16, tag="kt", align_bytes=64)
        gwf = gw[:].bitcast(F32).rearrange("p g (c u) -> p g c u", u=2)
        ww = w_raw[:].bitcast(F32)
        xc = {}
        xs = {}
        grp = {}
        kts = {}
        qts = {}

        def w_bank(c, eng):
            bank = transpose_mx(ww[:, c // 2, c % 2, :])
            evac(eng, gwf[:, :, P * c : P * (c + 1), :], bank[:].rearrange("p (g u) c -> p g c u", u=2))

        def w_quant(h):
            for g in range(2):
                nc.vector.quantize_mx(
                    out=wc[:, g, 512 * h : 512 * (h + 1)].bitcast(FP8X4),
                    scales=ws[:, g, 512 * h : 512 * (h + 1)],
                    in_=gw[:, g, 2048 * h : 2048 * (h + 1)],
                )

        ordered = {}

        def order(key, j, eng):
            words = work.tile([P, 2, 2, P], F32, tag="order", bufs=4)
            evac(eng, words[:], xraw[key][:].bitcast(F32)[:, j, :].rearrange("p (g w u) -> p g u w", g=2, u=2))
            ordered[key, j] = words

        def x_bank(key, j, eng):
            if j == 0:
                gt = gp.tile([P, 2, 4 * S], BF16, tag="g", align_bytes=64)
                grp[key] = gt
            gf = grp[key][:].bitcast(F32).rearrange("p g (c u) -> p g c u", u=2)
            if (key, j) in ordered:
                bank = transpose_words(ordered[key, j][:].rearrange("p g u w -> p (g u w)"))
            else:
                bank = transpose_mx(xraw[key][:].bitcast(F32)[:, j, :])
            evac(eng, gf[:, :, P * j : P * (j + 1), :], bank[:].rearrange("p (g u) c -> p g c u", u=2))

        def x_quant(key):
            xcb = codes.tile([P, 2, S], U32, name="xc" + key, align_bytes=64)
            xsb = codes.tile([P, 2, S], U8, name="xs" + key, align_bytes=64)
            xc[key] = xcb
            xs[key] = xsb

            def part(g):
                return lambda: nc.vector.quantize_mx(
                    out=xcb[:, g, :].bitcast(FP8X4), scales=xsb[:, g, :], in_=grp[key][:, g, :]
                )

            return [part(0), part(1)]

        def k_bank(b, tb, eng):
            if tb == 0:
                kt = ktp.tile([P, 8, KW], F32, tag="kt", align_bytes=64)
                nc.gpsimd.memset(kt[:, :, 0:KPAD], 0.0)
                nc.gpsimd.memset(kt[:, :, KPAD + S : KW], 0.0)
                kts[b] = kt
            bank = transpose_words(kraw[b][:].bitcast(F32)[:, tb, :])
            lo = KPAD + P * tb
            evac(
                eng,
                kts[b][:, :, lo : lo + P].rearrange("p (u e) k -> p u e k", e=2),
                bank[:].bitcast(BF16).rearrange("p u (k e) -> p u e k", e=2),
            )

        scv = sc[:, VS // P : VS // P + NV, :]
        vdone = [0]

        def mxv_group(r, h):
            key = "v%d" % (r // 4)
            cols = slice(P * (r % 4), P * (r % 4 + 1))
            qv = tp.tile([P, 512], F32, tag="tp")
            for g in range(2):
                nc.tensor.matmul_mx(
                    out=qv[:],
                    lhsT=xc[key][:, g, cols].bitcast(FP8X4),
                    lhsT_scale=xs[key][:, g, cols],
                    rhs=wc[:, g, 512 * h : 512 * (h + 1)].bitcast(FP8X4),
                    rhs_scale=ws[:, g, 512 * h : 512 * (h + 1)],
                    start=(g == 0),
                    stop=(g == 1),
                )
            nc.vector.tensor_tensor(
                out=qb[:, r, 512 * h : 512 * (h + 1)].rearrange("p (u q e) -> p u q e", u=2, e=2),
                in0=qv[:].rearrange("p (u e q) -> p u q e", u=2, e=2),
                in1=bb[:, 512 * h : 512 * (h + 1)].rearrange("p (u q e) -> p u q e", u=2, e=2),
                op=ALU.add,
            )

        def softmax(sc_t, groups, dests, label):
            mn = small.tile([P, groups], F32, name="mn" + label)
            ex = small.tile([P, groups, W5], F32, name="ex" + label)
            sm = small.tile([P, groups], F32, name="sm" + label)
            rs = small.tile([P, groups], F32, name="rs" + label)

            def shift():
                nc.vector.tensor_tensor(
                    out=sc_t, in0=sc_t, in1=mn[:].unsqueeze(2).to_broadcast([P, groups, W5]), op=ALU.subtract
                )
                nc.scalar.activation(out=ex[:], in_=sc_t, func=ACT.Exp, scale=-1.0)

            def scale():
                for g0, g1, dest in dests:
                    nc.vector.tensor_tensor(
                        out=dest,
                        in0=ex[:, g0:g1, :],
                        in1=rs[:, g0:g1].unsqueeze(2).to_broadcast([P, g1 - g0, W5]),
                        op=ALU.mult,
                    )

            return [
                lambda: nc.vector.tensor_reduce(out=mn[:], in_=sc_t, axis=AX.X, op=ALU.min),
                shift,
                lambda: nc.vector.tensor_reduce(out=sm[:], in_=ex[:], axis=AX.X, op=ALU.add),
                lambda: nc.vector.reciprocal(out=rs[:], in_=sm[:]),
                scale,
            ]

        def vfill(n):
            for i in range(n):
                if vdone[0] >= W5 * NV:
                    return
                r, j = divmod(vdone[0], W5)
                junk = work.tile([P, D], F32, tag="junk", bufs=2)
                nc.vector.scalar_tensor_tensor(
                    out=junk[:],
                    in0=qb[:, r, :],
                    scalar=-1.0 / 32.0,
                    in1=k_v[:, r + j, :],
                    op0=ALU.mult,
                    op1=ALU.mult,
                    accum_out=scv[:, r, j : j + 1],
                )
                vdone[0] += 1

        def mxp_group(b, c):
            key = "p%d" % b
            if c == 0:
                qt_sb = qtp.tile([P, 8, S], F32, tag="qt")
                qts[b] = qt_sb
            qt = tp.tile([P, 512], F32, tag="tp")
            for g in range(2):
                nc.tensor.matmul_mx(
                    out=qt[:],
                    lhsT=wc[:, g, P * c : P * (c + 1)].bitcast(FP8X4),
                    lhsT_scale=ws[:, g, P * c : P * (c + 1)],
                    rhs=xc[key][:, g, :].bitcast(FP8X4),
                    rhs_scale=xs[key][:, g, :],
                    start=(g == 0),
                    stop=(g == 1),
                )
            nc.scalar.activation(out=qts[b][:, c, :], in_=qt[:], func=ACT.Identity, bias=bpp[:, c : c + 1], scale=1.0)

        def new_scores():
            sps = sp.tile([P, 2, NWIN], F32, tag="s")
            return sps

        def score(b, tb, sps, at):
            lo = KPAD - 2 + P * tb
            for c in range(8):
                nc.tensor.matmul(
                    out=sps[:, at, :],
                    lhsT=qts[b][:, c, P * tb : P * (tb + 1)],
                    rhs=kts[b][:, c, lo : lo + NWIN],
                    start=(c == 0),
                    stop=(c == 7),
                )

        def extract(b, tb, n, sps):
            slot = 4 * b + tb
            bm = work.tile([P, 2, NWIN], F32, tag="bm")
            pr = work.tile([P, 2, W5, MOD + 1], F32, tag="pr")
            return [
                lambda: nc.vector.tensor_tensor(
                    out=bm[:, 0:n, :],
                    in0=sps[:, 0:n, :],
                    in1=band[:].unsqueeze(1).to_broadcast([P, n, NWIN]),
                    op=ALU.mult,
                ),
                lambda: nc.vector.tensor_reduce(
                    out=rr[:, slot : slot + n, 0:MOD],
                    in_=bm[:, 0:n, :].rearrange("p t (m r) -> p t r m", r=MOD),
                    axis=AX.X,
                    op=ALU.add,
                ),
                lambda: nc.vector.tensor_tensor(
                    out=pr[:, 0:n, :, :],
                    in0=rr[:, slot : slot + n, :].unsqueeze(2).to_broadcast([P, n, W5, MOD + 1]),
                    in1=sel[:, tb : tb + n, :, :],
                    op=ALU.mult,
                ),
                lambda: nc.vector.tensor_reduce(
                    out=sc[:, slot : slot + n, :], in_=pr[:, 0:n, :, :], axis=AX.X, op=ALU.add
                ),
            ]

        def weave(steps, others=()):
            others = list(others)
            for i, step in enumerate(steps):
                step()
                if i < len(others):
                    others[i]()
                elif i + 1 < len(steps):
                    vfill(1)
            for other in others[len(steps):]:
                other()

        ov = of.rearrange("(t p) j -> t (p j)", p=P)

        def turn(part):
            yp = ypads[part]
            ta = tp.tile([P, 4, P], F32, tag="tp")
            tb2 = tp.tile([P, 4, P], F32, tag="tp")
            for j in range(W5):
                nc.tensor.transpose(ta[:, j, :] if j < 3 else tb2[:, j - 3, :], yp[:, j, :], ident)
            zj = small.tile([P, W5, P], F32, name="zj" + part)
            nc.scalar.copy(out=zj[:, 3:5, :], in_=tb2[:, 0:2, :])
            if part == "a":
                nc.scalar.copy(out=zj[:, 0:3, :], in_=ta[:, 0:3, :])
            else:
                nc.vector.tensor_copy(out=zj[:, 0:3, :], in_=ta[:, 0:3, :])
            return zj

        for c in range(4):
            w_bank(c, "svsv"[c])
        bt = tp.tile([P, 4, P], F32, tag="tp")
        nc.tensor.transpose(bt[:, 0, :], brow[:].bitcast(F32), ident)
        bw = consts.tile([P, 4], F32)
        nc.vector.tensor_copy(out=bw[:], in_=bt[:, 0, 0:4])
        bpp = consts.tile([P, 8], F32)
        nc.vector.tensor_copy(out=bpp[:], in_=bw[:].bitcast(BF16))
        w_quant(0)
        for j in range(4):
            x_bank("p%d" % first, j, "svsv"[j])
        rep = work.tile([P, 4, P], F32, tag="order", bufs=4)
        nc.vector.tensor_copy(out=rep[:], in_=bw[:].unsqueeze(2).to_broadcast([P, 4, P]))
        for c in range(4, 6):
            w_bank(c, "ssss"[c - 4])
        for step in x_quant("p%d" % first):
            step()
        for c in range(6, 8):
            w_bank(c, "ssss"[c - 4])
        qb = rawp.tile([P, NV, D], F32, tag="big")
        for j in range(4):
            order("v0", j, "vvvv"[j])
        for c in range(4):
            mxp_group(first, c)
        w_quant(1)
        bbank = tp.tile([P, 4, P], F32, tag="tp")
        for u in range(4):
            nc.tensor.transpose(bbank[:, u, :], rep[:, u, :], ident)
        for j in range(4):
            x_bank("v0", j, "ssss"[j])
        bb = consts.tile([P, D], BF16)
        nc.vector.tensor_copy(out=bb[:].bitcast(F32), in_=bbank[:].rearrange("p u w -> p (u w)"))
        for step in x_quant("v0"):
            step()
        for c in range(4, 8):
            mxp_group(first, c)
        load_xp(third)
        for tb in range(4):
            k_bank(first, tb, "svsv"[tb])
        load_k(third)
        for r in range(4):
            for h in range(2):
                mxv_group(r, h)

        for b, nxt in ((first, second), (second, third), (third, None)):
            front = new_scores()
            score(b, 0, front, 0)
            if nxt is not None:
                for j in range(4):
                    order("p%d" % nxt, j, "s")
                if b == first:
                    masks()
                for j in range(2):
                    x_bank("p%d" % nxt, j, "s")
                vfill(2)
            score(b, 1, front, 1)
            if nxt is None:
                vfill(W5 * NV)
            if nxt is not None:
                for j in range(2, 4):
                    x_bank("p%d" % nxt, j, "s")
                vfill(1)
                k_bank(nxt, 0, "s")
            steps = extract(b, 0, 2, front)
            if nxt is not None:
                weave(steps, [lambda: vfill(1)] + x_quant("p%d" % nxt))
            else:
                weave(steps)
            back = new_scores()
            if nxt is not None:
                vfill(1)
                score(b, 2, back, 0)
                for tb in range(1, 4):
                    k_bank(nxt, tb, "s")
                for c in range(4):
                    mxp_group(nxt, c)
                score(b, 3, back, 1)
                for c in range(4, 8):
                    mxp_group(nxt, c)
                vfill(2)
                weave(extract(b, 2, 2, back))
                vfill(0)

        final = third
        score(final, 2, back, 0)
        vfill(W5 * NV)
        nc.vector.tensor_tensor(out=scv, in0=scv, in1=negv[:], op=ALU.add)
        ready = 4 * final + 2
        yv = small.tile([P, NV, W5], F32)
        ya = ypads["a"]
        early = softmax(
            sc[:, 0:ready, :],
            ready,
            (
                (0, 4, ya[:, :, 0:4].rearrange("p j t -> p t j")),
                (8, ready, ya[:, :, 8:ready].rearrange("p j t -> p t j")),
                (4, 8, yv[:]),
            ),
            "p",
        )
        weave(early, extract(final, 2, 1, back))
        nc.sync.dma_start(
            out=of[VS : VS + P * NV, :].rearrange("(p r) j -> p (r j)", r=NV), in_=yv[:].rearrange("p r j -> p (r j)")
        )
        lone = new_scores()
        score(final, 3, lone, 0)
        weave(extract(final, 3, 1, lone))
        low = small.tile([P, 2], F32)
        nc.vector.tensor_reduce(out=low[:], in_=sc[:, ready : ready + 2, :], axis=AX.X, op=ALU.min)
        exl = small.tile([P, 2, W5], F32)
        sml = small.tile([P, 2], F32)
        for i in range(2):
            nc.scalar.activation(
                out=exl[:, i, :],
                in_=sc[:, ready + i, :],
                func=ACT.Exp,
                bias=low[:, i : i + 1],
                scale=-1.0,
                accum_out=sml[:, i : i + 1],
            )
        rsl = small.tile([P, 2], F32)
        nc.vector.reciprocal(out=rsl[:], in_=sml[:])
        nc.vector.tensor_tensor(
            out=ypads["b"][:, :, 0:2].rearrange("p j t -> p t j"),
            in0=exl[:],
            in1=rsl[:].unsqueeze(2).to_broadcast([P, 2, W5]),
            op=ALU.mult,
        )
        zja = turn("a")
        za = small.tile([P, P, W5], F32)
        nc.vector.tensor_copy(out=za[:], in_=zja[:].rearrange("s j p -> s p j"))
        for b in PE_BATCHES:
            n = 4 if b != final else 2
            nc.sync.dma_start(out=ov[4 * b : 4 * b + n, :], in_=za[4 * b : 4 * b + n, :, :].rearrange("s p j -> s (p j)"))
        zjb = turn("b")
        zb = small.tile([P, P, W5], F32)
        nc.vector.tensor_copy(out=zb[:], in_=zjb[:].rearrange("s j p -> s p j"))
        nc.sync.dma_start(out=ov[ready : ready + 2, :], in_=zb[0:2, :, :].rearrange("s p j -> s (p j)"))
